import numpy as np
import ml_dtypes


def mxq(x, axis, fmt="e4m3"):
    dtype, down = {"e4m3": (ml_dtypes.float8_e4m3fn, 7), "e5m2": (ml_dtypes.float8_e5m2, 14)}[fmt]
    v = np.moveaxis(np.asarray(x, np.float32).astype(ml_dtypes.bfloat16).astype(np.float64), axis, -1)
    blocks = v.reshape(v.shape[:-1] + (-1, 32))
    amax = np.abs(blocks).max(-1, keepdims=True)
    byte = np.maximum(np.where(amax > 0, np.frexp(amax)[1] - 1 + 127, 0) - down, 1)
    scale = np.exp2(byte - 127.0)
    codes = (blocks / scale).astype(np.float32).astype(dtype).astype(np.float64)
    return np.moveaxis((codes * scale).reshape(v.shape), -1, axis)


WIDE = False


def mx_kscale(k):
    if not WIDE:
        return np.ones(k)
    levels = np.array([10, -10, 5, -5, 0])
    a = np.random.permutation(np.resize(levels, k // 512 * 4)).reshape(k // 512, 4)
    idx = np.arange(k)
    return np.exp2(a[idx // 512, idx % 128 // 32])


BF16 = ml_dtypes.bfloat16


def bf(x):
    return np.asarray(x, np.float32).astype(BF16)


def f64(x):
    return np.asarray(x).astype(np.float64)


B, N, D, DK, DV, HQ, WQ, HS, WS = 2, 16, 512, 512, 128, 16, 16, 16, 16
U = HQ * WQ
V = HS * WS
VS = 4.0 * np.sqrt(N) / U


def setup_inputs():
    s = mx_kscale(D)
    sc = s[None, :, None, None]
    offset = np.random.standard_normal((B, D))[:, :, None, None]
    return {"query": bf((np.random.standard_normal((B, D, HQ, WQ)) + offset) * sc),
            "support": bf(np.random.standard_normal((N, D, HS, WS)) * sc),
            "Wk": bf(np.random.standard_normal((DK, D)) / np.sqrt(D) / s[None, :]),
            "Wv": bf(np.random.standard_normal((DV, D)) * VS / np.sqrt(D) / s[None, :])}


def reference(query, support, Wk, Wv):
    qf = mxq(f64(query).reshape(B, D, U), 1, "e4m3")
    sf = mxq(f64(support).reshape(N, D, V), 1, "e4m3")
    wk = mxq(f64(Wk), 1, "e4m3")
    wv = mxq(f64(Wv), 1, "e4m3")
    q = wk @ qf
    support_key = wk @ sf
    support_value = wv @ sf
    scores = (mxq(q, 1, "e4m3").transpose(0, 2, 1)[:, None] @ mxq(support_key, 1, "e4m3")[None]) / np.sqrt(DK)
    e = np.exp(scores - scores.max(1, keepdims=True))
    attn = e / e.sum(1, keepdims=True)
    return (attn.sum(2)[:, :, None, :] * support_value[None]).sum(1)

@@ -1,0 +1,366 @@
+import math
+from contextlib import ExitStack
+
+import concourse.mybir as mybir
+from concourse.masks import make_identity
+
+F32 = mybir.dt.float32
+BF16 = mybir.dt.bfloat16
+U32 = mybir.dt.uint32
+U8 = mybir.dt.uint8
+FP8X4 = mybir.dt.float8_e4m3fn_x4
+ALU = mybir.AluOpType
+ACT = mybir.ActivationFunctionType
+
+P = 128
+NB = 2
+NS = 16
+FLOPS = 2 * 512 * 512 * 256 * (NB + NS) + 2 * 128 * 512 * 256 * NS + 2 * 512 * 256 * 256 * NB * NS
+
+HEAD_GROUPS = ((0, 4), (4, 4), (8, 4), (12, 2), (14, 2))
+LATE_GROUPS = ((0, 4), (4, 4), (8, 4), (12, 4))
+
+
+def tile_crossattention_pa_kernel(tc, query, support, Wk, Wv, out):
+    nc = tc.nc
+    with ExitStack() as ctx:
+        keep = ctx.enter_context(tc.tile_pool(name="keep", bufs=1))
+        stage = ctx.enter_context(tc.tile_pool(name="stage", bufs=3))
+        pair = ctx.enter_context(tc.tile_pool(name="pair", bufs=2))
+        psum = ctx.enter_context(tc.psum_pool(name="psum", bufs=2))
+        ctx.enter_context(tc.manual_schedule())
+
+        wk_sb = keep.tile([P, 2048], BF16, name="wk_sb")
+        nc.sync.dma_start(out=wk_sb[:], in_=Wk.rearrange("(p m) d -> p (m d)", m=4))
+        q_sb = keep.tile([P, NB, 1024], BF16, name="q_sb")
+        nc.sync.dma_start(out=q_sb[:], in_=query.rearrange("b (p j) h w -> p b (j h w)", j=4))
+        wv_sb = keep.tile([P, 512], BF16, name="wv_sb")
+        nc.sync.dma_start(out=wv_sb[:], in_=Wv)
+        sf_sb = keep.tile([P, NS, 1024], BF16, name="sf_sb")
+        for ch in range(8):
+            nc.sync.dma_start(
+                out=sf_sb[:, 2 * ch : 2 * ch + 2, :],
+                in_=support[2 * ch : 2 * ch + 2].rearrange("n (p j) h w -> p n (j h w)", j=4),
+            )
+
+        ident = keep.tile([P, P], F32, name="ident")
+        make_identity(nc, ident[:])
+        warm = keep.tile([P, 1], F32, name="warm")
+        nc.vector.memset(warm[:], 0.0)
+        nc.scalar.activation(out=warm[:], in_=warm[:], func=ACT.Exp)
+
+        def quantise(codes, scales, grouped):
+            nc.vector.quantize_mx(out=codes.bitcast(FP8X4), scales=scales, in_=grouped)
+
+        wk_w = wk_sb[:].bitcast(F32).rearrange("p (m w u) -> p m w u", m=4, u=2)
+        wkg = keep.tile([P, 2048], BF16, name="wkg", align_bytes=64)
+        wkg_w = wkg[:].bitcast(F32).rearrange("p (m c u) -> p m c u", m=4, u=2)
+        xts = []
+        for mp in range(2):
+            xt = psum.tile([P, 2, 2, P], F32, name="xt", tag="pj")
+            for mi in range(2):
+                for u in range(2):
+                    nc.tensor.transpose(xt[:, mi, u, :], wk_w[:, 2 * mp + mi, :, u], ident[:])
+            xts.append(xt)
+        nc.scalar.copy(out=wkg_w[:, 0:2, :, :], in_=xts[0][:].rearrange("p m u c -> p m c u"))
+        nc.vector.tensor_copy(out=wkg_w[:, 2:4, :, :], in_=xts[1][:].rearrange("p m u c -> p m c u"))
+        wkc = keep.tile([P, 512], U32, name="wkc", align_bytes=64)
+        wks = keep.tile([P, 512], U8, name="wks", align_bytes=64)
+        quantise(wkc[:], wks[:], wkg[:])
+
+        def project(codes, scales, blk, tag):
+            bank = psum.tile([P, 4, P], F32, name="pj", tag=tag, bufs=(4 if tag == "sc" else 2))
+            cols = slice(blk * P, (blk + 1) * P)
+            for m in range(4):
+                mc = slice(m * P, (m + 1) * P)
+                nc.tensor.matmul_mx(
+                    out=bank[:, m, :],
+                    lhsT=wkc[:, mc].bitcast(FP8X4),
+                    lhsT_scale=wks[:, mc],
+                    rhs=codes[:, cols].bitcast(FP8X4),
+                    rhs_scale=scales[:, cols],
+                    start=True,
+                    stop=True,
+                )
+            return bank
+
+        qg = keep.tile([P, 2048], BF16, name="qg", align_bytes=64)
+        qg_v = qg[:].rearrange("p (b c i t) -> p b c t i", b=NB, i=4, t=4)
+        for b in range(NB):
+            nc.vector.tensor_copy(
+                out=qg_v[:, b], in_=q_sb[:, b, :].rearrange("p (t c i) -> p c t i", t=4, i=4)
+            )
+        qfc = keep.tile([P, 512], U32, name="qfc", align_bytes=64)
+        qfs = keep.tile([P, 512], U8, name="qfs", align_bytes=64)
+        quantise(qfc[:], qfs[:], qg[:])
+        qpg = keep.tile([P, 2048], BF16, name="qpg", align_bytes=64)
+        qpg_v = qpg[:].rearrange("p (g w m) -> p g w m", g=4, m=4)
+        for g in range(4):
+            bank = project(qfc, qfs, g, "sc")
+            nc.scalar.copy(out=qpg_v[:, g], in_=bank[:].rearrange("p m w -> p w m"))
+        qc = keep.tile([P, 512], U32, name="qc", align_bytes=64)
+        qs = keep.tile([P, 512], U8, name="qs", align_bytes=64)
+
+        wv_w = wv_sb[:].bitcast(F32).rearrange("p (w u) -> p w u", u=2)
+        xv = psum.tile([P, 2, P], F32, name="xv", tag="pj")
+        for u in range(2):
+            nc.tensor.transpose(xv[:, u, :], wv_w[:, :, u], ident[:])
+        wvg = keep.tile([P, 512], BF16, name="wvg", align_bytes=64)
+        nc.scalar.copy(
+            out=wvg[:].bitcast(F32).rearrange("p (c u) -> p c u", u=2),
+            in_=xv[:].rearrange("p u c -> p c u"),
+        )
+        wvc = keep.tile([P, P], U32, name="wvc", align_bytes=64)
+        wvs = keep.tile([P, P], U8, name="wvs", align_bytes=64)
+
+        sfc = [keep.tile([P, 2048], U32, name="sfc%d" % vc, align_bytes=64) for vc in range(2)]
+        sfs = [keep.tile([P, 2048], U8, name="sfs%d" % vc, align_bytes=64) for vc in range(2)]
+        kc = [keep.tile([P, 2048], U32, name="kc%d" % vc, align_bytes=64) for vc in range(2)]
+        ks = [keep.tile([P, 2048], U8, name="ks%d" % vc, align_bytes=64) for vc in range(2)]
+
+        def quantise_support(vc, n0, cnt):
+            sfg = stage.tile([P, cnt * 512], BF16, name="sfg", tag="sfg", align_bytes=64)
+            sfg_v = sfg[:].rearrange("p (n c i t) -> p n c t i", n=cnt, i=4, t=4)
+            for nl in range(cnt):
+                src = sf_sb[:, n0 + nl, :].rearrange("p (t w c i) -> p w c t i", t=4, w=2, i=4)
+                nc.vector.tensor_copy(out=sfg_v[:, nl], in_=src[:, vc])
+            cols = slice(n0 * P, (n0 + cnt) * P)
+            quantise(sfc[vc][:, cols], sfs[vc][:, cols], sfg[:])
+
+        def project_keys(vc, n0, cnt, tag):
+            kg = stage.tile([P, cnt * 512], BF16, name="kg", tag="kg", align_bytes=64)
+            kg_v = kg[:].rearrange("p (g w m) -> p g w m", g=cnt, m=4)
+            for nl in range(cnt):
+                bank = project(sfc[vc], sfs[vc], n0 + nl, tag)
+                nc.scalar.copy(out=kg_v[:, nl], in_=bank[:].rearrange("p m w -> p w m"))
+            return kg
+
+        def quantise_keys(vc, n0, cnt, kg):
+            cols = slice(n0 * P, (n0 + cnt) * P)
+            quantise(kc[vc][:, cols], ks[vc][:, cols], kg[:])
+
+        kgs = {}
+        for g in range(len(HEAD_GROUPS)):
+            n0, cnt = HEAD_GROUPS[g]
+            quantise_support(0, n0, cnt)
+            if g == 1:
+                quantise(qc[:], qs[:], qpg[:])
+            if g == 2:
+                quantise(wvc[:], wvs[:], wvg[:])
+            if g >= 1:
+                quantise_keys(0, HEAD_GROUPS[g - 1][0], HEAD_GROUPS[g - 1][1], kgs[g - 1])
+            kgs[g] = project_keys(0, n0, cnt, "sc")
+        quantise_keys(0, HEAD_GROUPS[-1][0], HEAD_GROUPS[-1][1], kgs[len(HEAD_GROUPS) - 1])
+
+        vt = [keep.tile([P, NS, P], F32, name="vt%d" % vc) for vc in range(2)]
+
+        def values(vc, g):
+            bank = psum.tile([P, 4, P], F32, name="vb", tag="pj")
+            for i in range(4):
+                cols = slice((4 * g + i) * P, (4 * g + i + 1) * P)
+                nc.tensor.matmul_mx(
+                    out=bank[:, i, :],
+                    lhsT=sfc[vc][:, cols].bitcast(FP8X4),
+                    lhsT_scale=sfs[vc][:, cols],
+                    rhs=wvc[:].bitcast(FP8X4),
+                    rhs_scale=wvs[:],
+                    start=True,
+                    stop=True,
+                )
+            nc.scalar.copy(out=vt[vc][:, 4 * g : 4 * g + 4, :], in_=bank[:])
+
+        ssum = keep.tile([P, 4 * NS], F32, name="ssum")
+        inv_sqrt = 1.0 / math.sqrt(512.0)
+        banks = {}
+        c0s = {}
+        es = {}
+        rs = {}
+        zts = {}
+        BANK_ORDER = (1, 2, 3, 0)
+
+        def scores(i):
+            vc, b, uh = i // 4, (i // 2) % 2, i % 2
+            qcols = slice((2 * b + uh) * P, (2 * b + uh + 1) * P)
+            banks[i] = []
+            for j in range(4):
+                bank = psum.tile([P, 4, P], F32, name="sc", tag="sc", bufs=4)
+                for a in range(4):
+                    cols = slice((4 * j + a) * P, (4 * j + a + 1) * P)
+                    nc.tensor.matmul_mx(
+                        out=bank[:, a, :],
+                        lhsT=kc[vc][:, cols].bitcast(FP8X4),
+                        lhsT_scale=ks[vc][:, cols],
+                        rhs=qc[:, qcols].bitcast(FP8X4),
+                        rhs_scale=qs[:, qcols],
+                        start=True,
+                        stop=True,
+                    )
+                banks[i].append(bank)
+
+        def copy_bank0(i):
+            c0 = pair.tile([P, 4, P], F32, name="c0", tag="c0")
+            nc.scalar.copy(out=c0[:], in_=banks[i][0][:])
+            c0s[i] = c0
+
+        def max_and_subtract(i):
+            k, uh = i // 2, i % 2
+            if uh == 0:
+                es[k] = pair.tile([P, NS, 256], F32, name="e", tag="e")
+                rs[k] = pair.tile([P, 256], F32, name="r", tag="r")
+            e = es[k]
+            us = slice(uh * P, (uh + 1) * P)
+            bk = banks[i]
+            t4 = pair.tile([P, 4, P], F32, name="t4", tag="t4")
+            nc.vector.tensor_tensor(out=t4[:], in0=bk[1][:], in1=c0s[i][:], op=ALU.max)
+            nc.vector.tensor_tensor(out=t4[:], in0=bk[2][:], in1=t4[:], op=ALU.max)
+            nc.vector.tensor_tensor(out=t4[:], in0=bk[3][:], in1=t4[:], op=ALU.max)
+            t2 = pair.tile([P, 2, P], F32, name="t2", tag="t2")
+            nc.vector.tensor_tensor(out=t2[:], in0=t4[:, 0:2, :], in1=t4[:, 2:4, :], op=ALU.max)
+            mx = pair.tile([P, P], F32, name="mx", tag="mx")
+            nc.vector.tensor_tensor(out=mx[:], in0=t2[:, 0, :], in1=t2[:, 1, :], op=ALU.max)
+            mx_b = mx[:].unsqueeze(1).to_broadcast([P, 4, P])
+            nc.gpsimd.tensor_tensor(out=e[:, 0:4, us], in0=c0s[i][:], in1=mx_b, op=ALU.subtract)
+            for j in range(1, 4):
+                nc.vector.tensor_tensor(
+                    out=e[:, 4 * j : 4 * j + 4, us], in0=bk[j][:], in1=mx_b, op=ALU.subtract
+                )
+
+        def exponentials(i):
+            e = es[i // 2]
+            us = slice((i % 2) * P, (i % 2 + 1) * P)
+            for j in BANK_ORDER:
+                nc.scalar.activation(
+                    out=e[:, 4 * j : 4 * j + 4, us],
+                    in_=e[:, 4 * j : 4 * j + 4, us],
+                    func=ACT.Exp,
+                    scale=inv_sqrt,
+                )
+
+        def sum_over_images(i):
+            e = es[i // 2]
+            us = slice((i % 2) * P, (i % 2 + 1) * P)
+            zt = psum.tile([P, P], F32, name="zt", tag="z")
+            order = [4 * j + a for j in BANK_ORDER for a in range(4)]
+            for pos in range(NS):
+                nc.tensor.matmul(
+                    out=zt[:],
+                    lhsT=e[:, order[pos], us],
+                    rhs=ident[:],
+                    is_transpose=True,
+                    start=(pos == 0),
+                    stop=(pos == NS - 1),
+                )
+            zts[i] = zt
+
+        rts = {}
+
+        def reciprocal(i):
+            rt = pair.tile([P, P], F32, name="rt", tag="rt")
+            nc.vector.reciprocal(out=rt[:], in_=zts[i][:])
+            rts[i] = rt
+
+        def reciprocal_back(i):
+            us = slice((i % 2) * P, (i % 2 + 1) * P)
+            rp = psum.tile([P, P], F32, name="rp", tag="z")
+            nc.tensor.transpose(rp[:], rts[i][:], ident[:])
+            nc.scalar.copy(out=rs[i // 2][:, us], in_=rp[:])
+
+        def weigh(w):
+            k, h = w // 2, w % 2
+            e = es[k]
+            for n in range(8 * h, 8 * h + 8):
+                col = k * NS + n
+                nc.vector.scalar_tensor_tensor(
+                    out=e[:, n, :],
+                    in0=e[:, n, :],
+                    scalar=1.0,
+                    in1=rs[k][:],
+                    op0=ALU.mult,
+                    op1=ALU.mult,
+                    accum_out=ssum[:, col : col + 1],
+                )
+
+        prods = {}
+
+        def products(k, on_vector):
+            vc = k // 2
+            prod = pair.tile([P, NS, P], F32, name="prod", tag="prod")
+            if on_vector:
+                for n in range(NS):
+                    col = k * NS + n
+                    nc.vector.tensor_scalar(
+                        out=prod[:, n, :],
+                        in0=vt[vc][:, n, :],
+                        scalar1=ssum[:, col : col + 1],
+                        scalar2=None,
+                        op0=ALU.mult,
+                    )
+            else:
+                nc.gpsimd.tensor_tensor(
+                    out=prod[:],
+                    in0=vt[vc][:],
+                    in1=ssum[:, k * NS : (k + 1) * NS].unsqueeze(2).to_broadcast([P, NS, P]),
+                    op=ALU.mult,
+                )
+            prods[k] = prod
+
+        def finish(k):
+            vc, b = k // 2, k % 2
+            res = psum.tile([P, P], F32, name="res", tag="pj")
+            for n in range(NS):
+                nc.tensor.matmul(
+                    out=res[:],
+                    lhsT=prods[k][:, n, :],
+                    rhs=ident[:],
+                    is_transpose=True,
+                    start=(n == 0),
+                    stop=(n == NS - 1),
+                )
+            ot = pair.tile([P, P], F32, name="ot", tag="ot")
+            nc.scalar.copy(out=ot[:], in_=res[:])
+            nc.sync.dma_start(out=out[b, :, vc * P : (vc + 1) * P], in_=ot[:])
+
+        late = {}
+        scores(0)
+        copy_bank0(0)
+        for i in range(8):
+            max_and_subtract(i)
+            if i < 7:
+                scores(i + 1)
+            exponentials(i)
+            if i < 7:
+                copy_bank0(i + 1)
+            sum_over_images(i)
+            if i < 2:
+                quantise_support(1, LATE_GROUPS[2 * i][0], 4)
+                quantise_support(1, LATE_GROUPS[2 * i + 1][0], 4)
+            else:
+                weigh(i - 2)
+            reciprocal(i)
+            if i == 0:
+                for g in range(4):
+                    values(0, g)
+                late[0] = project_keys(1, 0, 4, "pj")
+            if i == 1:
+                late[1] = project_keys(1, 4, 4, "pj")
+                late[2] = project_keys(1, 8, 4, "pj")
+            if i == 2:
+                late[3] = project_keys(1, 12, 4, "pj")
+                for g in range(4):
+                    values(1, g)
+            reciprocal_back(i)
+            if i == 1:
+                quantise_keys(1, 0, 4, late[0])
+            if i == 2:
+                for g in range(1, 4):
+                    quantise_keys(1, 4 * g, 4, late[g])
+            if i == 3 or i == 5:
+                products((i - 3) // 2, False)
+            if i == 4 or i == 6:
+                finish((i - 4) // 2)
+        products(2, True)
+        finish(2)
+        weigh(6)
+        weigh(7)
+        products(3, True)
+        finish(3)

@@ -11,6 +11,7 @@ U8 = mybir.dt.uint8
 FP8X4 = mybir.dt.float8_e4m3fn_x4
 ALU = mybir.AluOpType
 ACT = mybir.ActivationFunctionType
+AX = mybir.AxisListType
 
 P = 128
 NB = 2
@@ -18,7 +19,11 @@ NS = 16
 FLOPS = 2 * 512 * 512 * 256 * (NB + NS) + 2 * 128 * 512 * 256 * NS + 2 * 512 * 256 * 256 * NB * NS
 
 HEAD_GROUPS = ((0, 4), (4, 4), (8, 4), (12, 2), (14, 2))
-LATE_GROUPS = ((0, 4), (4, 4), (8, 4), (12, 4))
+G_BANKS = (0,)
+S_REGROUP = False
+G_MULT_UNITS = 7
+G_MULT = (1,)
+V_EVAC = (3, 4)
 
 
 def tile_crossattention_pa_kernel(tc, query, support, Wk, Wv, out):
@@ -28,7 +33,6 @@ def tile_crossattention_pa_kernel(tc, query, support, Wk, Wv, out):
         stage = ctx.enter_context(tc.tile_pool(name="stage", bufs=3))
         pair = ctx.enter_context(tc.tile_pool(name="pair", bufs=2))
         psum = ctx.enter_context(tc.psum_pool(name="psum", bufs=2))
-        ctx.enter_context(tc.manual_schedule())
 
         wk_sb = keep.tile([P, 2048], BF16, name="wk_sb")
         nc.sync.dma_start(out=wk_sb[:], in_=Wk.rearrange("(p m) d -> p (m d)", m=4))
@@ -48,6 +52,10 @@ def tile_crossattention_pa_kernel(tc, query, support, Wk, Wv, out):
         warm = keep.tile([P, 1], F32, name="warm")
         nc.vector.memset(warm[:], 0.0)
         nc.scalar.activation(out=warm[:], in_=warm[:], func=ACT.Exp)
+        sel = keep.tile([P, NS], F32, name="sel")
+        nc.vector.tensor_reduce(
+            out=sel[:], in_=ident[:].rearrange("p (n j) -> p n j", j=8), axis=AX.X, op=ALU.add
+        )
 
         def quantise(codes, scales, grouped):
             nc.vector.quantize_mx(out=codes.bitcast(FP8X4), scales=scales, in_=grouped)
@@ -84,12 +92,45 @@ def tile_crossattention_pa_kernel(tc, query, support, Wk, Wv, out):
                 )
             return bank
 
+        sfc = [keep.tile([P, 2048], U32, name="sfc%d" % vc, align_bytes=64) for vc in range(2)]
+        sfs = [keep.tile([P, 2048], U8, name="sfs%d" % vc, align_bytes=64) for vc in range(2)]
+        kc = [keep.tile([P, 2048], U32, name="kc%d" % vc, align_bytes=64) for vc in range(2)]
+        ks = [keep.tile([P, 2048], U8, name="ks%d" % vc, align_bytes=64) for vc in range(2)]
+
+        def quantise_support(vc, n0, cnt):
+            sfg = stage.tile([P, cnt * 512], BF16, name="sfg", tag="sfg", align_bytes=64)
+            src = sf_sb[:, n0 : n0 + cnt, :].rearrange("p n (t w c i) -> p w n c t i", t=4, w=2, i=4)
+            if vc == 1 and S_REGROUP:
+                nc.scalar.copy(
+                    out=sfg[:].rearrange("p (n c i t) -> p n c t i", n=cnt, i=4, t=4), in_=src[:, vc]
+                )
+            else:
+                nc.vector.tensor_copy(
+                    out=sfg[:].rearrange("p (n c i t) -> p n c t i", n=cnt, i=4, t=4), in_=src[:, vc]
+                )
+            cols = slice(n0 * P, (n0 + cnt) * P)
+            quantise(sfc[vc][:, cols], sfs[vc][:, cols], sfg[:])
+
+        def project_keys(vc, n0, cnt, tag, vector_last):
+            kg = stage.tile([P, cnt * 512], BF16, name="kg", tag="kg", align_bytes=64)
+            kg_v = kg[:].rearrange("p (g w m) -> p g w m", g=cnt, m=4)
+            for nl in range(cnt):
+                bank = project(sfc[vc], sfs[vc], n0 + nl, tag)
+                if vector_last and nl == cnt - 1:
+                    nc.vector.tensor_copy(out=kg_v[:, nl], in_=bank[:].rearrange("p m w -> p w m"))
+                else:
+                    nc.scalar.copy(out=kg_v[:, nl], in_=bank[:].rearrange("p m w -> p w m"))
+            return kg
+
+        def quantise_keys(vc, n0, cnt, kg):
+            cols = slice(n0 * P, (n0 + cnt) * P)
+            quantise(kc[vc][:, cols], ks[vc][:, cols], kg[:])
+
         qg = keep.tile([P, 2048], BF16, name="qg", align_bytes=64)
-        qg_v = qg[:].rearrange("p (b c i t) -> p b c t i", b=NB, i=4, t=4)
-        for b in range(NB):
-            nc.vector.tensor_copy(
-                out=qg_v[:, b], in_=q_sb[:, b, :].rearrange("p (t c i) -> p c t i", t=4, i=4)
-            )
+        nc.vector.tensor_copy(
+            out=qg[:].rearrange("p (b c i t) -> p b c t i", b=NB, i=4, t=4),
+            in_=q_sb[:].rearrange("p b (t c i) -> p b c t i", t=4, i=4),
+        )
         qfc = keep.tile([P, 512], U32, name="qfc", align_bytes=64)
         qfs = keep.tile([P, 512], U8, name="qfs", align_bytes=64)
         quantise(qfc[:], qfs[:], qg[:])
@@ -113,44 +154,18 @@ def tile_crossattention_pa_kernel(tc, query, support, Wk, Wv, out):
         wvc = keep.tile([P, P], U32, name="wvc", align_bytes=64)
         wvs = keep.tile([P, P], U8, name="wvs", align_bytes=64)
 
-        sfc = [keep.tile([P, 2048], U32, name="sfc%d" % vc, align_bytes=64) for vc in range(2)]
-        sfs = [keep.tile([P, 2048], U8, name="sfs%d" % vc, align_bytes=64) for vc in range(2)]
-        kc = [keep.tile([P, 2048], U32, name="kc%d" % vc, align_bytes=64) for vc in range(2)]
-        ks = [keep.tile([P, 2048], U8, name="ks%d" % vc, align_bytes=64) for vc in range(2)]
-
-        def quantise_support(vc, n0, cnt):
-            sfg = stage.tile([P, cnt * 512], BF16, name="sfg", tag="sfg", align_bytes=64)
-            sfg_v = sfg[:].rearrange("p (n c i t) -> p n c t i", n=cnt, i=4, t=4)
-            for nl in range(cnt):
-                src = sf_sb[:, n0 + nl, :].rearrange("p (t w c i) -> p w c t i", t=4, w=2, i=4)
-                nc.vector.tensor_copy(out=sfg_v[:, nl], in_=src[:, vc])
-            cols = slice(n0 * P, (n0 + cnt) * P)
-            quantise(sfc[vc][:, cols], sfs[vc][:, cols], sfg[:])
-
-        def project_keys(vc, n0, cnt, tag):
-            kg = stage.tile([P, cnt * 512], BF16, name="kg", tag="kg", align_bytes=64)
-            kg_v = kg[:].rearrange("p (g w m) -> p g w m", g=cnt, m=4)
-            for nl in range(cnt):
-                bank = project(sfc[vc], sfs[vc], n0 + nl, tag)
-                nc.scalar.copy(out=kg_v[:, nl], in_=bank[:].rearrange("p m w -> p w m"))
-            return kg
-
-        def quantise_keys(vc, n0, cnt, kg):
-            cols = slice(n0 * P, (n0 + cnt) * P)
-            quantise(kc[vc][:, cols], ks[vc][:, cols], kg[:])
-
         kgs = {}
-        for g in range(len(HEAD_GROUPS)):
-            n0, cnt = HEAD_GROUPS[g]
-            quantise_support(0, n0, cnt)
+        ng = len(HEAD_GROUPS)
+        for g in range(ng + 2):
+            if g < ng:
+                n0, cnt = HEAD_GROUPS[g]
+                quantise_support(0, n0, cnt)
+                kgs[g] = project_keys(0, n0, cnt, "sc", g in V_EVAC)
             if g == 1:
                 quantise(qc[:], qs[:], qpg[:])
-            if g == 2:
-                quantise(wvc[:], wvs[:], wvg[:])
-            if g >= 1:
-                quantise_keys(0, HEAD_GROUPS[g - 1][0], HEAD_GROUPS[g - 1][1], kgs[g - 1])
-            kgs[g] = project_keys(0, n0, cnt, "sc")
-        quantise_keys(0, HEAD_GROUPS[-1][0], HEAD_GROUPS[-1][1], kgs[len(HEAD_GROUPS) - 1])
+            if g >= 2:
+                quantise_keys(0, HEAD_GROUPS[g - 2][0], HEAD_GROUPS[g - 2][1], kgs[g - 2])
+        quantise(wvc[:], wvs[:], wvg[:])
 
         vt = [keep.tile([P, NS, P], F32, name="vt%d" % vc) for vc in range(2)]
 
@@ -169,20 +184,24 @@ def tile_crossattention_pa_kernel(tc, query, support, Wk, Wv, out):
                 )
             nc.scalar.copy(out=vt[vc][:, 4 * g : 4 * g + 4, :], in_=bank[:])
 
-        ssum = keep.tile([P, 4 * NS], F32, name="ssum")
         inv_sqrt = 1.0 / math.sqrt(512.0)
         banks = {}
-        c0s = {}
+        cps = {}
         es = {}
         rs = {}
         zts = {}
-        BANK_ORDER = (1, 2, 3, 0)
+        rts = {}
+        atts = {}
+        p1s = {}
+        prods = {}
+        BANK_ORDER = (0, 1, 2, 3)
 
-        def scores(i):
+        def scores(i, js):
             vc, b, uh = i // 4, (i // 2) % 2, i % 2
             qcols = slice((2 * b + uh) * P, (2 * b + uh + 1) * P)
-            banks[i] = []
-            for j in range(4):
+            if 0 in js:
+                banks[i] = []
+            for j in js:
                 bank = psum.tile([P, 4, P], F32, name="sc", tag="sc", bufs=4)
                 for a in range(4):
                     cols = slice((4 * j + a) * P, (4 * j + a + 1) * P)
@@ -197,54 +216,69 @@ def tile_crossattention_pa_kernel(tc, query, support, Wk, Wv, out):
                     )
                 banks[i].append(bank)
 
-        def copy_bank0(i):
-            c0 = pair.tile([P, 4, P], F32, name="c0", tag="c0")
-            nc.scalar.copy(out=c0[:], in_=banks[i][0][:])
-            c0s[i] = c0
+        def copy_banks(i):
+            cps[i] = {}
+            for j in G_BANKS:
+                cp = pair.tile([P, 4, P], F32, name="cp%d" % j, tag="cp%d" % j)
+                nc.scalar.copy(out=cp[:], in_=banks[i][j][:])
+                cps[i][j] = cp
 
-        def max_and_subtract(i):
-            k, uh = i // 2, i % 2
-            if uh == 0:
-                es[k] = pair.tile([P, NS, 256], F32, name="e", tag="e")
-                rs[k] = pair.tile([P, 256], F32, name="r", tag="r")
-            e = es[k]
-            us = slice(uh * P, (uh + 1) * P)
+        mxs = {}
+
+        def maximum(i):
+            e = pair.tile([P, NS, P], F32, name="e", tag="e", bufs=3)
+            es[i] = e
             bk = banks[i]
+            cp = cps[i]
             t4 = pair.tile([P, 4, P], F32, name="t4", tag="t4")
-            nc.vector.tensor_tensor(out=t4[:], in0=bk[1][:], in1=c0s[i][:], op=ALU.max)
-            nc.vector.tensor_tensor(out=t4[:], in0=bk[2][:], in1=t4[:], op=ALU.max)
-            nc.vector.tensor_tensor(out=t4[:], in0=bk[3][:], in1=t4[:], op=ALU.max)
+            if len(G_BANKS) == 1:
+                nc.vector.tensor_tensor(out=t4[:], in0=bk[1][:], in1=cp[0][:], op=ALU.max)
+                nc.vector.tensor_tensor(out=t4[:], in0=bk[2][:], in1=t4[:], op=ALU.max)
+                nc.vector.tensor_tensor(out=t4[:], in0=bk[3][:], in1=t4[:], op=ALU.max)
+            else:
+                t4b = pair.tile([P, 4, P], F32, name="t4b", tag="t4b")
+                nc.vector.tensor_tensor(out=t4[:], in0=bk[1][:], in1=cp[0][:], op=ALU.max)
+                nc.vector.tensor_tensor(out=t4b[:], in0=bk[3][:], in1=cp[2][:], op=ALU.max)
+                nc.vector.tensor_tensor(out=t4[:], in0=t4[:], in1=t4b[:], op=ALU.max)
             t2 = pair.tile([P, 2, P], F32, name="t2", tag="t2")
             nc.vector.tensor_tensor(out=t2[:], in0=t4[:, 0:2, :], in1=t4[:, 2:4, :], op=ALU.max)
             mx = pair.tile([P, P], F32, name="mx", tag="mx")
             nc.vector.tensor_tensor(out=mx[:], in0=t2[:, 0, :], in1=t2[:, 1, :], op=ALU.max)
-            mx_b = mx[:].unsqueeze(1).to_broadcast([P, 4, P])
-            nc.gpsimd.tensor_tensor(out=e[:, 0:4, us], in0=c0s[i][:], in1=mx_b, op=ALU.subtract)
-            for j in range(1, 4):
-                nc.vector.tensor_tensor(
-                    out=e[:, 4 * j : 4 * j + 4, us], in0=bk[j][:], in1=mx_b, op=ALU.subtract
+            mxs[i] = mx
+
+        def subtract(i, on_gpsimd):
+            e = es[i]
+            bk = banks[i]
+            cp = cps[i]
+            mx_b = mxs[i][:].unsqueeze(1).to_broadcast([P, 4, P])
+            for j in G_BANKS if on_gpsimd else ():
+                nc.gpsimd.tensor_tensor(
+                    out=e[:, 4 * j : 4 * j + 4, :], in0=cp[j][:], in1=mx_b, op=ALU.subtract
                 )
+            for j in () if on_gpsimd else range(4):
+                if j not in G_BANKS:
+                    nc.vector.tensor_tensor(
+                        out=e[:, 4 * j : 4 * j + 4, :], in0=bk[j][:], in1=mx_b, op=ALU.subtract
+                    )
 
         def exponentials(i):
-            e = es[i // 2]
-            us = slice((i % 2) * P, (i % 2 + 1) * P)
+            e = es[i]
             for j in BANK_ORDER:
                 nc.scalar.activation(
-                    out=e[:, 4 * j : 4 * j + 4, us],
-                    in_=e[:, 4 * j : 4 * j + 4, us],
+                    out=e[:, 4 * j : 4 * j + 4, :],
+                    in_=e[:, 4 * j : 4 * j + 4, :],
                     func=ACT.Exp,
                     scale=inv_sqrt,
                 )
 
         def sum_over_images(i):
-            e = es[i // 2]
-            us = slice((i % 2) * P, (i % 2 + 1) * P)
-            zt = psum.tile([P, P], F32, name="zt", tag="z")
+            e = es[i]
+            zt = psum.tile([P, P], F32, name="zt", tag="z", bufs=1)
             order = [4 * j + a for j in BANK_ORDER for a in range(4)]
             for pos in range(NS):
                 nc.tensor.matmul(
                     out=zt[:],
-                    lhsT=e[:, order[pos], us],
+                    lhsT=e[:, order[pos], :],
                     rhs=ident[:],
                     is_transpose=True,
                     start=(pos == 0),
@@ -252,57 +286,81 @@ def tile_crossattention_pa_kernel(tc, query, support, Wk, Wv, out):
                 )
             zts[i] = zt
 
-        rts = {}
-
         def reciprocal(i):
             rt = pair.tile([P, P], F32, name="rt", tag="rt")
             nc.vector.reciprocal(out=rt[:], in_=zts[i][:])
             rts[i] = rt
 
         def reciprocal_back(i):
-            us = slice((i % 2) * P, (i % 2 + 1) * P)
-            rp = psum.tile([P, P], F32, name="rp", tag="z")
+            rp = psum.tile([P, P], F32, name="rp", tag="z", bufs=1)
             nc.tensor.transpose(rp[:], rts[i][:], ident[:])
-            nc.scalar.copy(out=rs[i // 2][:, us], in_=rp[:])
+            r = pair.tile([P, P], F32, name="r", tag="r")
+            nc.scalar.copy(out=r[:], in_=rp[:])
+            rs[i] = r
 
-        def weigh(w):
-            k, h = w // 2, w % 2
-            e = es[k]
-            for n in range(8 * h, 8 * h + 8):
-                col = k * NS + n
-                nc.vector.scalar_tensor_tensor(
-                    out=e[:, n, :],
-                    in0=e[:, n, :],
-                    scalar=1.0,
-                    in1=rs[k][:],
-                    op0=ALU.mult,
-                    op1=ALU.mult,
-                    accum_out=ssum[:, col : col + 1],
+        def multiply(i, h):
+            if h == 0:
+                atts[i] = pair.tile([P, 16, NS, 8], F32, name="att", tag="att")
+            eng = nc.gpsimd if (h in G_MULT and i < G_MULT_UNITS) else nc.vector
+            us = slice(64 * h, 64 * h + 64)
+            eng.tensor_tensor(
+                out=atts[i][:, 8 * h : 8 * h + 8, :, :],
+                in0=es[i][:, :, us].rearrange("p n (g j) -> p g n j", j=8),
+                in1=rs[i][:, us]
+                .rearrange("p (g j) -> p g j", j=8)
+                .unsqueeze(2)
+                .to_broadcast([P, 8, NS, 8]),
+                op=ALU.mult,
+            )
+
+        def add_blocks(i):
+            k, uh = i // 2, i % 2
+            if uh == 0:
+                p1s[k] = psum.tile([P, P], F32, name="p1", tag="acc", bufs=1)
+            for g in range(16):
+                nc.tensor.matmul(
+                    out=p1s[k][:],
+                    lhsT=atts[i][:, g, :, :].rearrange("p n j -> p (n j)"),
+                    rhs=ident[:],
+                    is_transpose=True,
+                    start=(uh == 0 and g == 0),
+                    stop=(uh == 1 and g == 15),
                 )
 
-        prods = {}
+        ssums = {}
 
-        def products(k, on_vector):
+        def sums_of_pair(k):
+            p1 = pair.tile([P, P], F32, name="p1s", tag="p1s")
+            nc.scalar.copy(out=p1[:], in_=p1s[k][:])
+            sp = psum.tile([P, NS], F32, name="sp", tag="pj")
+            nc.tensor.matmul(out=sp[:], lhsT=p1[:], rhs=sel[:], start=True, stop=True)
+            ssum = pair.tile([P, NS], F32, name="ssum", tag="ssum")
+            nc.scalar.copy(out=ssum[:], in_=sp[:])
+            ssums[k] = ssum
+
+        def products(k, half, on_vector):
             vc = k // 2
-            prod = pair.tile([P, NS, P], F32, name="prod", tag="prod")
+            ssum = ssums[k]
+            if half == 0:
+                prods[k] = pair.tile([P, NS, P], F32, name="prod", tag="prod")
+            prod = prods[k]
+            ns = slice(8 * half, 8 * half + 8)
             if on_vector:
-                for n in range(NS):
-                    col = k * NS + n
+                for n in range(8 * half, 8 * half + 8):
                     nc.vector.tensor_scalar(
                         out=prod[:, n, :],
                         in0=vt[vc][:, n, :],
-                        scalar1=ssum[:, col : col + 1],
+                        scalar1=ssum[:, n : n + 1],
                         scalar2=None,
                         op0=ALU.mult,
                     )
             else:
                 nc.gpsimd.tensor_tensor(
-                    out=prod[:],
-                    in0=vt[vc][:],
-                    in1=ssum[:, k * NS : (k + 1) * NS].unsqueeze(2).to_broadcast([P, NS, P]),
+                    out=prod[:, ns, :],
+                    in0=vt[vc][:, ns, :],
+                    in1=ssum[:, ns].unsqueeze(2).to_broadcast([P, 8, P]),
                     op=ALU.mult,
                 )
-            prods[k] = prod
 
         def finish(k):
             vc, b = k // 2, k % 2
@@ -321,46 +379,50 @@ def tile_crossattention_pa_kernel(tc, query, support, Wk, Wv, out):
             nc.sync.dma_start(out=out[b, :, vc * P : (vc + 1) * P], in_=ot[:])
 
         late = {}
-        scores(0)
-        copy_bank0(0)
-        for i in range(8):
-            max_and_subtract(i)
-            if i < 7:
-                scores(i + 1)
-            exponentials(i)
-            if i < 7:
-                copy_bank0(i + 1)
-            sum_over_images(i)
+        EARLY = tuple(range(0, max(G_BANKS) + 1))
+        REST = tuple(range(max(G_BANKS) + 1, 4))
+        scores(0, EARLY)
+        copy_banks(0)
+        scores(0, REST)
+        for i in range(10):
+            if i + 1 < 8:
+                scores(i + 1, EARLY)
+                copy_banks(i + 1)
+            if i >= 3 and i % 2 == 1:
+                sums_of_pair((i - 3) // 2)
+            if i >= 5 and i % 2 == 1:
+                finish((i - 5) // 2)
+            if 1 <= i <= 2:
+                for g in (2 * i - 2, 2 * i - 1):
+                    late[g] = project_keys(1, 4 * g, 4, "pj", False)
+            if 3 <= i < 7:
+                for g in (0, 1):
+                    values((i - 3) // 2, 2 * ((i - 3) % 2) + g)
+            if i < 8:
+                maximum(i)
+                subtract(i, True)
+            if 1 <= i <= 8:
+                reciprocal(i - 1)
+                reciprocal_back(i - 1)
+            if i < 8:
+                subtract(i, False)
+            if i + 1 < 8:
+                scores(i + 1, REST)
+            if i < 8:
+                exponentials(i)
+                sum_over_images(i)
             if i < 2:
-                quantise_support(1, LATE_GROUPS[2 * i][0], 4)
-                quantise_support(1, LATE_GROUPS[2 * i + 1][0], 4)
-            else:
-                weigh(i - 2)
-            reciprocal(i)
-            if i == 0:
-                for g in range(4):
-                    values(0, g)
-                late[0] = project_keys(1, 0, 4, "pj")
-            if i == 1:
-                late[1] = project_keys(1, 4, 4, "pj")
-                late[2] = project_keys(1, 8, 4, "pj")
-            if i == 2:
-                late[3] = project_keys(1, 12, 4, "pj")
-                for g in range(4):
-                    values(1, g)
-            reciprocal_back(i)
-            if i == 1:
-                quantise_keys(1, 0, 4, late[0])
-            if i == 2:
-                for g in range(1, 4):
+                quantise_support(1, 8 * i, 4)
+                quantise_support(1, 8 * i + 4, 4)
+            if 1 <= i <= 8:
+                multiply(i - 1, 0)
+                multiply(i - 1, 1)
+                add_blocks(i - 1)
+            if i == 1 or i == 2:
+                for g in (2 * i - 2, 2 * i - 1):
                     quantise_keys(1, 4 * g, 4, late[g])
-            if i == 3 or i == 5:
-                products((i - 3) // 2, False)
-            if i == 4 or i == 6:
-                finish((i - 4) // 2)
-        products(2, True)
-        finish(2)
-        weigh(6)
-        weigh(7)
-        products(3, True)
+            if 3 <= i < 9:
+                products((i - 3) // 2, (i - 3) % 2, False)
+        products(3, 0, True)
+        products(3, 1, True)
         finish(3)

@@ -22,8 +22,8 @@ HEAD_GROUPS = ((0, 4), (4, 4), (8, 4), (12, 2), (14, 2))
 G_BANKS = (0,)
 S_REGROUP = False
 G_MULT_UNITS = 7
-G_MULT = (1,)
-V_EVAC = (3, 4)
+G_MULT = ()
+V_EVAC = ()
 
 
 def tile_crossattention_pa_kernel(tc, query, support, Wk, Wv, out):
@@ -33,6 +33,7 @@ def tile_crossattention_pa_kernel(tc, query, support, Wk, Wv, out):
         stage = ctx.enter_context(tc.tile_pool(name="stage", bufs=3))
         pair = ctx.enter_context(tc.tile_pool(name="pair", bufs=2))
         psum = ctx.enter_context(tc.psum_pool(name="psum", bufs=2))
+        ctx.enter_context(tc.manual_schedule())
 
         wk_sb = keep.tile([P, 2048], BF16, name="wk_sb")
         nc.sync.dma_start(out=wk_sb[:], in_=Wk.rearrange("(p m) d -> p (m d)", m=4))
@@ -77,7 +78,7 @@ def tile_crossattention_pa_kernel(tc, query, support, Wk, Wv, out):
         quantise(wkc[:], wks[:], wkg[:])
 
         def project(codes, scales, blk, tag):
-            bank = psum.tile([P, 4, P], F32, name="pj", tag=tag, bufs=(4 if tag == "sc" else 2))
+            bank = psum.tile([P, 4, P], F32, name="pj", tag=tag, bufs=(3 if tag == "sc" else 2))
             cols = slice(blk * P, (blk + 1) * P)
             for m in range(4):
                 mc = slice(m * P, (m + 1) * P)
@@ -202,7 +203,10 @@ def tile_crossattention_pa_kernel(tc, query, support, Wk, Wv, out):
             if 0 in js:
                 banks[i] = []
             for j in js:
-                bank = psum.tile([P, 4, P], F32, name="sc", tag="sc", bufs=4)
+                if j in G_BANKS:
+                    bank = psum.tile([P, 4, P], F32, name="s0", tag="pj")
+                else:
+                    bank = psum.tile([P, 4, P], F32, name="sc", tag="sc", bufs=3)
                 for a in range(4):
                     cols = slice((4 * j + a) * P, (4 * j + a + 1) * P)
                     nc.tensor.matmul_mx(
@@ -292,11 +296,9 @@ def tile_crossattention_pa_kernel(tc, query, support, Wk, Wv, out):
             rts[i] = rt
 
         def reciprocal_back(i):
-            rp = psum.tile([P, P], F32, name="rp", tag="z", bufs=1)
+            rp = psum.tile([P, P], F32, name="rp", tag="rp", bufs=1)
             nc.tensor.transpose(rp[:], rts[i][:], ident[:])
-            r = pair.tile([P, P], F32, name="r", tag="r")
-            nc.scalar.copy(out=r[:], in_=rp[:])
-            rs[i] = r
+            rs[i] = rp
 
         def multiply(i, h):
             if h == 0:

@@ -20,9 +20,10 @@ FLOPS = 2 * 512 * 512 * 256 * (NB + NS) + 2 * 128 * 512 * 256 * NS + 2 * 512 * 2
 
 HEAD_GROUPS = ((0, 4), (4, 4), (8, 4), (12, 2), (14, 2))
 G_BANKS = (0,)
+S_PROD = 0
 S_REGROUP = False
 G_MULT_UNITS = 7
-G_MULT = ()
+G_MULT = (1,)
 V_EVAC = ()
 
 
@@ -72,10 +73,9 @@ def tile_crossattention_pa_kernel(tc, query, support, Wk, Wv, out):
                     nc.tensor.transpose(xt[:, mi, u, :], wk_w[:, 2 * mp + mi, :, u], ident[:])
             xts.append(xt)
         nc.scalar.copy(out=wkg_w[:, 0:2, :, :], in_=xts[0][:].rearrange("p m u c -> p m c u"))
-        nc.vector.tensor_copy(out=wkg_w[:, 2:4, :, :], in_=xts[1][:].rearrange("p m u c -> p m c u"))
+        nc.scalar.copy(out=wkg_w[:, 2:4, :, :], in_=xts[1][:].rearrange("p m u c -> p m c u"))
         wkc = keep.tile([P, 512], U32, name="wkc", align_bytes=64)
         wks = keep.tile([P, 512], U8, name="wks", align_bytes=64)
-        quantise(wkc[:], wks[:], wkg[:])
 
         def project(codes, scales, blk, tag):
             bank = psum.tile([P, 4, P], F32, name="pj", tag=tag, bufs=(3 if tag == "sc" else 2))
@@ -132,6 +132,7 @@ def tile_crossattention_pa_kernel(tc, query, support, Wk, Wv, out):
             out=qg[:].rearrange("p (b c i t) -> p b c t i", b=NB, i=4, t=4),
             in_=q_sb[:].rearrange("p b (t c i) -> p b c t i", t=4, i=4),
         )
+        quantise(wkc[:], wks[:], wkg[:])
         qfc = keep.tile([P, 512], U32, name="qfc", align_bytes=64)
         qfs = keep.tile([P, 512], U8, name="qfs", align_bytes=64)
         quantise(qfc[:], qfs[:], qg[:])
@@ -164,6 +165,8 @@ def tile_crossattention_pa_kernel(tc, query, support, Wk, Wv, out):
                 kgs[g] = project_keys(0, n0, cnt, "sc", g in V_EVAC)
             if g == 1:
                 quantise(qc[:], qs[:], qpg[:])
+            if g >= ng:
+                quantise_support(1, 4 * (g - ng), 4)
             if g >= 2:
                 quantise_keys(0, HEAD_GROUPS[g - 2][0], HEAD_GROUPS[g - 2][1], kgs[g - 2])
         quantise(wvc[:], wvs[:], wvg[:])
@@ -241,8 +244,8 @@ def tile_crossattention_pa_kernel(tc, query, support, Wk, Wv, out):
                 nc.vector.tensor_tensor(out=t4[:], in0=bk[3][:], in1=t4[:], op=ALU.max)
             else:
                 t4b = pair.tile([P, 4, P], F32, name="t4b", tag="t4b")
-                nc.vector.tensor_tensor(out=t4[:], in0=bk[1][:], in1=cp[0][:], op=ALU.max)
-                nc.vector.tensor_tensor(out=t4b[:], in0=bk[3][:], in1=cp[2][:], op=ALU.max)
+                nc.vector.tensor_tensor(out=t4[:], in0=bk[2][:], in1=cp[0][:], op=ALU.max)
+                nc.vector.tensor_tensor(out=t4b[:], in0=bk[3][:], in1=cp[1][:], op=ALU.max)
                 nc.vector.tensor_tensor(out=t4[:], in0=t4[:], in1=t4b[:], op=ALU.max)
             t2 = pair.tile([P, 2, P], F32, name="t2", tag="t2")
             nc.vector.tensor_tensor(out=t2[:], in0=t4[:, 0:2, :], in1=t4[:, 2:4, :], op=ALU.max)
@@ -295,31 +298,38 @@ def tile_crossattention_pa_kernel(tc, query, support, Wk, Wv, out):
             nc.vector.reciprocal(out=rt[:], in_=zts[i][:])
             rts[i] = rt
 
+        rbs = {}
+
         def reciprocal_back(i):
             rp = psum.tile([P, P], F32, name="rp", tag="rp", bufs=1)
             nc.tensor.transpose(rp[:], rts[i][:], ident[:])
             rs[i] = rp
+            if G_MULT and i < G_MULT_UNITS:
+                rb = pair.tile([P, 64], F32, name="rb", tag="rb")
+                nc.scalar.copy(out=rb[:], in_=rp[:, 64:128])
+                rbs[i] = rb
 
         def multiply(i, h):
             if h == 0:
                 atts[i] = pair.tile([P, 16, NS, 8], F32, name="att", tag="att")
-            eng = nc.gpsimd if (h in G_MULT and i < G_MULT_UNITS) else nc.vector
+            on_g = h in G_MULT and i < G_MULT_UNITS
+            eng = nc.gpsimd if on_g else nc.vector
             us = slice(64 * h, 64 * h + 64)
             eng.tensor_tensor(
                 out=atts[i][:, 8 * h : 8 * h + 8, :, :],
                 in0=es[i][:, :, us].rearrange("p n (g j) -> p g n j", j=8),
-                in1=rs[i][:, us]
+                in1=(rbs[i][:] if on_g else rs[i][:, us])
                 .rearrange("p (g j) -> p g j", j=8)
                 .unsqueeze(2)
                 .to_broadcast([P, 8, NS, 8]),
                 op=ALU.mult,
             )
 
-        def add_blocks(i):
+        def add_blocks(i, h):
             k, uh = i // 2, i % 2
-            if uh == 0:
+            if uh == 0 and h == 0:
                 p1s[k] = psum.tile([P, P], F32, name="p1", tag="acc", bufs=1)
-            for g in range(16):
+            for g in range(8 * h, 8 * h + 8):
                 nc.tensor.matmul(
                     out=p1s[k][:],
                     lhsT=atts[i][:, g, :, :].rearrange("p n j -> p (n j)"),
@@ -357,12 +367,18 @@ def tile_crossattention_pa_kernel(tc, query, support, Wk, Wv, out):
                         op0=ALU.mult,
                     )
             else:
+                ng_ = 8 - S_PROD
+                ns = slice(8 * half, 8 * half + ng_)
                 nc.gpsimd.tensor_tensor(
                     out=prod[:, ns, :],
                     in0=vt[vc][:, ns, :],
-                    in1=ssum[:, ns].unsqueeze(2).to_broadcast([P, 8, P]),
+                    in1=ssum[:, ns].unsqueeze(2).to_broadcast([P, ng_, P]),
                     op=ALU.mult,
                 )
+                for n in range(8 * half + ng_, 8 * half + 8):
+                    nc.scalar.activation(
+                        out=prod[:, n, :], in_=vt[vc][:, n, :], func=ACT.Copy, scale=ssum[:, n : n + 1]
+                    )
 
         def finish(k):
             vc, b = k // 2, k % 2
@@ -386,16 +402,16 @@ def tile_crossattention_pa_kernel(tc, query, support, Wk, Wv, out):
         scores(0, EARLY)
         copy_banks(0)
         scores(0, REST)
-        for i in range(10):
+        for i in range(11):
             if i + 1 < 8:
                 scores(i + 1, EARLY)
                 copy_banks(i + 1)
-            if i >= 3 and i % 2 == 1:
-                sums_of_pair((i - 3) // 2)
-            if i >= 5 and i % 2 == 1:
-                finish((i - 5) // 2)
-            if 1 <= i <= 2:
-                for g in (2 * i - 2, 2 * i - 1):
+            if i >= 4 and i % 2 == 0:
+                sums_of_pair((i - 4) // 2)
+            if i >= 6 and i % 2 == 0:
+                finish((i - 6) // 2)
+            if i <= 1:
+                for g in (2 * i, 2 * i + 1):
                     late[g] = project_keys(1, 4 * g, 4, "pj", False)
             if 3 <= i < 7:
                 for g in (0, 1):
@@ -403,28 +419,29 @@ def tile_crossattention_pa_kernel(tc, query, support, Wk, Wv, out):
             if i < 8:
                 maximum(i)
                 subtract(i, True)
-            if 1 <= i <= 8:
-                reciprocal(i - 1)
-                reciprocal_back(i - 1)
-            if i < 8:
                 subtract(i, False)
             if i + 1 < 8:
                 scores(i + 1, REST)
             if i < 8:
                 exponentials(i)
-                sum_over_images(i)
-            if i < 2:
-                quantise_support(1, 8 * i, 4)
-                quantise_support(1, 8 * i + 4, 4)
+            if i == 0:
+                quantise_support(1, 8, 4)
+                quantise_support(1, 12, 4)
+            if 2 <= i < 10:
+                multiply(i - 2, 0)
+                multiply(i - 2, 1)
+                add_blocks(i - 2, 0)
+                add_blocks(i - 2, 1)
             if 1 <= i <= 8:
-                multiply(i - 1, 0)
-                multiply(i - 1, 1)
-                add_blocks(i - 1)
-            if i == 1 or i == 2:
-                for g in (2 * i - 2, 2 * i - 1):
+                reciprocal(i - 1)
+                reciprocal_back(i - 1)
+            if i < 8:
+                sum_over_images(i)
+            if i <= 1:
+                for g in (2 * i, 2 * i + 1):
                     quantise_keys(1, 4 * g, 4, late[g])
-            if 3 <= i < 9:
-                products((i - 3) // 2, (i - 3) % 2, False)
+            if 4 <= i < 10:
+                products((i - 4) // 2, i % 2, False)
         products(3, 0, True)
         products(3, 1, True)
         finish(3)

@@ -14,17 +14,20 @@ ACT = mybir.ActivationFunctionType
 AX = mybir.AxisListType
 
 P = 128
+PACK = 4
 NB = 2
 NS = 16
+GROUP = 4
+GROUPS = NS // GROUP
+UNITS = 8
+PAIRS = UNITS // 2
+TAIL = 8
 FLOPS = 2 * 512 * 512 * 256 * (NB + NS) + 2 * 128 * 512 * 256 * NS + 2 * 512 * 256 * 256 * NB * NS
 
-HEAD_GROUPS = ((0, 4), (4, 4), (8, 4), (12, 2), (14, 2))
-G_BANKS = (0,)
-S_PROD = 0
-S_REGROUP = False
-G_MULT_UNITS = 7
-G_MULT = (1,)
-V_EVAC = ()
+
+def pair_due(slot, lag):
+    pair, rest = divmod(slot - lag, 2)
+    return pair if rest == 0 and 0 <= pair < PAIRS else None
 
 
 def tile_crossattention_pa_kernel(tc, query, support, Wk, Wv, out):
@@ -32,21 +35,21 @@ def tile_crossattention_pa_kernel(tc, query, support, Wk, Wv, out):
     with ExitStack() as ctx:
         keep = ctx.enter_context(tc.tile_pool(name="keep", bufs=1))
         stage = ctx.enter_context(tc.tile_pool(name="stage", bufs=3))
-        pair = ctx.enter_context(tc.tile_pool(name="pair", bufs=2))
+        work = ctx.enter_context(tc.tile_pool(name="work", bufs=2))
         psum = ctx.enter_context(tc.psum_pool(name="psum", bufs=2))
         ctx.enter_context(tc.manual_schedule())
 
-        wk_sb = keep.tile([P, 2048], BF16, name="wk_sb")
-        nc.sync.dma_start(out=wk_sb[:], in_=Wk.rearrange("(p m) d -> p (m d)", m=4))
-        q_sb = keep.tile([P, NB, 1024], BF16, name="q_sb")
-        nc.sync.dma_start(out=q_sb[:], in_=query.rearrange("b (p j) h w -> p b (j h w)", j=4))
+        wk_sb = keep.tile([P, PACK * 512], BF16, name="wk_sb")
+        nc.sync.dma_start(out=wk_sb[:], in_=Wk.rearrange("(p m) d -> p (m d)", m=PACK))
+        q_sb = keep.tile([P, NB, PACK * 256], BF16, name="q_sb")
+        nc.sync.dma_start(out=q_sb[:], in_=query.rearrange("b (p j) h w -> p b (j h w)", j=PACK))
         wv_sb = keep.tile([P, 512], BF16, name="wv_sb")
         nc.sync.dma_start(out=wv_sb[:], in_=Wv)
-        sf_sb = keep.tile([P, NS, 1024], BF16, name="sf_sb")
-        for ch in range(8):
+        sf_sb = keep.tile([P, NS, PACK * 256], BF16, name="sf_sb")
+        for n in range(0, NS, 2):
             nc.sync.dma_start(
-                out=sf_sb[:, 2 * ch : 2 * ch + 2, :],
-                in_=support[2 * ch : 2 * ch + 2].rearrange("n (p j) h w -> p n (j h w)", j=4),
+                out=sf_sb[:, n : n + 2, :],
+                in_=support[n : n + 2].rearrange("n (p j) h w -> p n (j h w)", j=PACK),
             )
 
         ident = keep.tile([P, P], F32, name="ident")
@@ -54,38 +57,45 @@ def tile_crossattention_pa_kernel(tc, query, support, Wk, Wv, out):
         warm = keep.tile([P, 1], F32, name="warm")
         nc.vector.memset(warm[:], 0.0)
         nc.scalar.activation(out=warm[:], in_=warm[:], func=ACT.Exp)
-        sel = keep.tile([P, NS], F32, name="sel")
+        same_image = keep.tile([P, NS], F32, name="same_image")
         nc.vector.tensor_reduce(
-            out=sel[:], in_=ident[:].rearrange("p (n j) -> p n j", j=8), axis=AX.X, op=ALU.add
+            out=same_image[:], in_=ident[:].rearrange("p (n j) -> p n j", j=TAIL), axis=AX.X, op=ALU.add
         )
 
         def quantise(codes, scales, grouped):
             nc.vector.quantize_mx(out=codes.bitcast(FP8X4), scales=scales, in_=grouped)
 
-        wk_w = wk_sb[:].bitcast(F32).rearrange("p (m w u) -> p m w u", m=4, u=2)
-        wkg = keep.tile([P, 2048], BF16, name="wkg", align_bytes=64)
-        wkg_w = wkg[:].bitcast(F32).rearrange("p (m c u) -> p m c u", m=4, u=2)
-        xts = []
-        for mp in range(2):
-            xt = psum.tile([P, 2, 2, P], F32, name="xt", tag="pj")
-            for mi in range(2):
-                for u in range(2):
-                    nc.tensor.transpose(xt[:, mi, u, :], wk_w[:, 2 * mp + mi, :, u], ident[:])
-            xts.append(xt)
-        nc.scalar.copy(out=wkg_w[:, 0:2, :, :], in_=xts[0][:].rearrange("p m u c -> p m c u"))
-        nc.scalar.copy(out=wkg_w[:, 2:4, :, :], in_=xts[1][:].rearrange("p m u c -> p m c u"))
-        wkc = keep.tile([P, 512], U32, name="wkc", align_bytes=64)
-        wks = keep.tile([P, 512], U8, name="wks", align_bytes=64)
+        def packed(name, columns):
+            codes = keep.tile([P, columns], U32, name=name + "_codes", align_bytes=64)
+            scales = keep.tile([P, columns], U8, name=name + "_scales", align_bytes=64)
+            return codes, scales
 
-        def project(codes, scales, blk, tag):
-            bank = psum.tile([P, 4, P], F32, name="pj", tag=tag, bufs=(3 if tag == "sc" else 2))
-            cols = slice(blk * P, (blk + 1) * P)
-            for m in range(4):
-                mc = slice(m * P, (m + 1) * P)
+        wk_words = wk_sb[:].bitcast(F32).rearrange("p (m w u) -> p m w u", m=PACK, u=2)
+        wk_grouped = keep.tile([P, PACK * 512], BF16, name="wk_grouped", align_bytes=64)
+        wk_grouped_words = wk_grouped[:].bitcast(F32).rearrange("p (m c u) -> p m c u", m=PACK, u=2)
+        turned = []
+        for first in (0, 2):
+            bank = psum.tile([P, 2, 2, P], F32, name="wk_turned", tag="short")
+            for m in range(2):
+                for u in range(2):
+                    nc.tensor.transpose(bank[:, m, u, :], wk_words[:, first + m, :, u], ident[:])
+            turned.append(bank)
+        for first in (0, 2):
+            nc.scalar.copy(
+                out=wk_grouped_words[:, first : first + 2, :, :],
+                in_=turned[first // 2][:].rearrange("p m u c -> p m c u"),
+            )
+        wk_codes, wk_scales = packed("wk", 512)
+
+        def project(codes, scales, block, tag):
+            bank = psum.tile([P, PACK, P], F32, name="projected", tag=tag, bufs=(3 if tag == "scores" else 2))
+            cols = slice(block * P, (block + 1) * P)
+            for m in range(PACK):
+                chunk = slice(m * P, (m + 1) * P)
                 nc.tensor.matmul_mx(
                     out=bank[:, m, :],
-                    lhsT=wkc[:, mc].bitcast(FP8X4),
-                    lhsT_scale=wks[:, mc],
+                    lhsT=wk_codes[:, chunk].bitcast(FP8X4),
+                    lhsT_scale=wk_scales[:, chunk],
                     rhs=codes[:, cols].bitcast(FP8X4),
                     rhs_scale=scales[:, cols],
                     start=True,
@@ -93,355 +103,304 @@ def tile_crossattention_pa_kernel(tc, query, support, Wk, Wv, out):
                 )
             return bank
 
-        sfc = [keep.tile([P, 2048], U32, name="sfc%d" % vc, align_bytes=64) for vc in range(2)]
-        sfs = [keep.tile([P, 2048], U8, name="sfs%d" % vc, align_bytes=64) for vc in range(2)]
-        kc = [keep.tile([P, 2048], U32, name="kc%d" % vc, align_bytes=64) for vc in range(2)]
-        ks = [keep.tile([P, 2048], U8, name="ks%d" % vc, align_bytes=64) for vc in range(2)]
+        def round_and_group(grouped, bank):
+            nc.scalar.copy(out=grouped, in_=bank[:].rearrange("p m w -> p w m"))
 
-        def quantise_support(vc, n0, cnt):
-            sfg = stage.tile([P, cnt * 512], BF16, name="sfg", tag="sfg", align_bytes=64)
-            src = sf_sb[:, n0 : n0 + cnt, :].rearrange("p n (t w c i) -> p w n c t i", t=4, w=2, i=4)
-            if vc == 1 and S_REGROUP:
-                nc.scalar.copy(
-                    out=sfg[:].rearrange("p (n c i t) -> p n c t i", n=cnt, i=4, t=4), in_=src[:, vc]
-                )
-            else:
-                nc.vector.tensor_copy(
-                    out=sfg[:].rearrange("p (n c i t) -> p n c t i", n=cnt, i=4, t=4), in_=src[:, vc]
-                )
-            cols = slice(n0 * P, (n0 + cnt) * P)
-            quantise(sfc[vc][:, cols], sfs[vc][:, cols], sfg[:])
+        sf_packed = [packed("sf%d" % half, NS * P) for half in range(2)]
+        key_packed = [packed("key%d" % half, NS * P) for half in range(2)]
 
-        def project_keys(vc, n0, cnt, tag, vector_last):
-            kg = stage.tile([P, cnt * 512], BF16, name="kg", tag="kg", align_bytes=64)
-            kg_v = kg[:].rearrange("p (g w m) -> p g w m", g=cnt, m=4)
-            for nl in range(cnt):
-                bank = project(sfc[vc], sfs[vc], n0 + nl, tag)
-                if vector_last and nl == cnt - 1:
-                    nc.vector.tensor_copy(out=kg_v[:, nl], in_=bank[:].rearrange("p m w -> p w m"))
-                else:
-                    nc.scalar.copy(out=kg_v[:, nl], in_=bank[:].rearrange("p m w -> p w m"))
-            return kg
+        def quantise_support(half, group):
+            n0 = group * GROUP
+            grouped = stage.tile([P, GROUP * P * PACK], BF16, name="sf_grouped", tag="sf_grouped", align_bytes=64)
+            rows = sf_sb[:, n0 : n0 + GROUP, :].rearrange("p n (t h c i) -> p h n c t i", t=PACK, h=2, i=4)
+            nc.vector.tensor_copy(
+                out=grouped[:].rearrange("p (n c i t) -> p n c t i", n=GROUP, i=4, t=PACK), in_=rows[:, half]
+            )
+            cols = slice(n0 * P, (n0 + GROUP) * P)
+            quantise(sf_packed[half][0][:, cols], sf_packed[half][1][:, cols], grouped[:])
 
-        def quantise_keys(vc, n0, cnt, kg):
-            cols = slice(n0 * P, (n0 + cnt) * P)
-            quantise(kc[vc][:, cols], ks[vc][:, cols], kg[:])
+        def project_keys(half, group, tag):
+            grouped = stage.tile([P, GROUP * P * PACK], BF16, name="key_grouped", tag="key_grouped", align_bytes=64)
+            by_image = grouped[:].rearrange("p (g w m) -> p g w m", g=GROUP, m=PACK)
+            for g in range(GROUP):
+                bank = project(sf_packed[half][0], sf_packed[half][1], group * GROUP + g, tag)
+                round_and_group(by_image[:, g], bank)
+            return grouped
 
-        qg = keep.tile([P, 2048], BF16, name="qg", align_bytes=64)
+        def quantise_keys(half, group, grouped):
+            cols = slice(group * GROUP * P, (group + 1) * GROUP * P)
+            quantise(key_packed[half][0][:, cols], key_packed[half][1][:, cols], grouped[:])
+
+        qf_grouped = keep.tile([P, NB * 256 * PACK], BF16, name="qf_grouped", align_bytes=64)
         nc.vector.tensor_copy(
-            out=qg[:].rearrange("p (b c i t) -> p b c t i", b=NB, i=4, t=4),
-            in_=q_sb[:].rearrange("p b (t c i) -> p b c t i", t=4, i=4),
+            out=qf_grouped[:].rearrange("p (b c i t) -> p b c t i", b=NB, i=4, t=PACK),
+            in_=q_sb[:].rearrange("p b (t c i) -> p b c t i", t=PACK, i=4),
         )
-        quantise(wkc[:], wks[:], wkg[:])
-        qfc = keep.tile([P, 512], U32, name="qfc", align_bytes=64)
-        qfs = keep.tile([P, 512], U8, name="qfs", align_bytes=64)
-        quantise(qfc[:], qfs[:], qg[:])
-        qpg = keep.tile([P, 2048], BF16, name="qpg", align_bytes=64)
-        qpg_v = qpg[:].rearrange("p (g w m) -> p g w m", g=4, m=4)
-        for g in range(4):
-            bank = project(qfc, qfs, g, "sc")
-            nc.scalar.copy(out=qpg_v[:, g], in_=bank[:].rearrange("p m w -> p w m"))
-        qc = keep.tile([P, 512], U32, name="qc", align_bytes=64)
-        qs = keep.tile([P, 512], U8, name="qs", align_bytes=64)
+        quantise(wk_codes[:], wk_scales[:], wk_grouped[:])
+        qf_codes, qf_scales = packed("qf", NB * 256)
+        quantise(qf_codes[:], qf_scales[:], qf_grouped[:])
+        q_grouped = keep.tile([P, NB * 256 * PACK], BF16, name="q_grouped", align_bytes=64)
+        q_by_block = q_grouped[:].rearrange("p (g w m) -> p g w m", g=2 * NB, m=PACK)
+        for block in range(2 * NB):
+            round_and_group(q_by_block[:, block], project(qf_codes, qf_scales, block, "scores"))
+        q_codes, q_scales = packed("q", NB * 256)
 
-        wv_w = wv_sb[:].bitcast(F32).rearrange("p (w u) -> p w u", u=2)
-        xv = psum.tile([P, 2, P], F32, name="xv", tag="pj")
+        wv_words = wv_sb[:].bitcast(F32).rearrange("p (w u) -> p w u", u=2)
+        wv_turned = psum.tile([P, 2, P], F32, name="wv_turned", tag="short")
         for u in range(2):
-            nc.tensor.transpose(xv[:, u, :], wv_w[:, :, u], ident[:])
-        wvg = keep.tile([P, 512], BF16, name="wvg", align_bytes=64)
+            nc.tensor.transpose(wv_turned[:, u, :], wv_words[:, :, u], ident[:])
+        wv_grouped = keep.tile([P, P * PACK], BF16, name="wv_grouped", align_bytes=64)
         nc.scalar.copy(
-            out=wvg[:].bitcast(F32).rearrange("p (c u) -> p c u", u=2),
-            in_=xv[:].rearrange("p u c -> p c u"),
+            out=wv_grouped[:].bitcast(F32).rearrange("p (c u) -> p c u", u=2),
+            in_=wv_turned[:].rearrange("p u c -> p c u"),
         )
-        wvc = keep.tile([P, P], U32, name="wvc", align_bytes=64)
-        wvs = keep.tile([P, P], U8, name="wvs", align_bytes=64)
+        wv_codes, wv_scales = packed("wv", P)
 
-        kgs = {}
-        ng = len(HEAD_GROUPS)
-        for g in range(ng + 2):
-            if g < ng:
-                n0, cnt = HEAD_GROUPS[g]
-                quantise_support(0, n0, cnt)
-                kgs[g] = project_keys(0, n0, cnt, "sc", g in V_EVAC)
-            if g == 1:
-                quantise(qc[:], qs[:], qpg[:])
-            if g >= ng:
-                quantise_support(1, 4 * (g - ng), 4)
-            if g >= 2:
-                quantise_keys(0, HEAD_GROUPS[g - 2][0], HEAD_GROUPS[g - 2][1], kgs[g - 2])
-        quantise(wvc[:], wvs[:], wvg[:])
+        key_grouped = {}
+        for turn in range(GROUPS + 2):
+            if turn < GROUPS:
+                quantise_support(0, turn)
+                key_grouped[turn] = project_keys(0, turn, "scores")
+            if turn == 1:
+                quantise(q_codes[:], q_scales[:], q_grouped[:])
+            if turn >= GROUPS:
+                quantise_support(1, turn - GROUPS)
+            if turn >= 2:
+                quantise_keys(0, turn - 2, key_grouped[turn - 2])
+        quantise(wv_codes[:], wv_scales[:], wv_grouped[:])
 
-        vt = [keep.tile([P, NS, P], F32, name="vt%d" % vc) for vc in range(2)]
+        val_t = [keep.tile([P, NS, P], F32, name="val_t%d" % half) for half in range(2)]
 
-        def values(vc, g):
-            bank = psum.tile([P, 4, P], F32, name="vb", tag="pj")
-            for i in range(4):
-                cols = slice((4 * g + i) * P, (4 * g + i + 1) * P)
+        def values(half, group):
+            bank = psum.tile([P, GROUP, P], F32, name="val_bank", tag="short")
+            for g in range(GROUP):
+                cols = slice((group * GROUP + g) * P, (group * GROUP + g + 1) * P)
                 nc.tensor.matmul_mx(
-                    out=bank[:, i, :],
-                    lhsT=sfc[vc][:, cols].bitcast(FP8X4),
-                    lhsT_scale=sfs[vc][:, cols],
-                    rhs=wvc[:].bitcast(FP8X4),
-                    rhs_scale=wvs[:],
+                    out=bank[:, g, :],
+                    lhsT=sf_packed[half][0][:, cols].bitcast(FP8X4),
+                    lhsT_scale=sf_packed[half][1][:, cols],
+                    rhs=wv_codes[:].bitcast(FP8X4),
+                    rhs_scale=wv_scales[:],
                     start=True,
                     stop=True,
                 )
-            nc.scalar.copy(out=vt[vc][:, 4 * g : 4 * g + 4, :], in_=bank[:])
+            nc.scalar.copy(out=val_t[half][:, group * GROUP : (group + 1) * GROUP, :], in_=bank[:])
 
         inv_sqrt = 1.0 / math.sqrt(512.0)
         banks = {}
-        cps = {}
-        es = {}
-        rs = {}
-        zts = {}
-        rts = {}
-        atts = {}
-        p1s = {}
-        prods = {}
-        BANK_ORDER = (0, 1, 2, 3)
+        bank0_copy = {}
+        maxima = {}
+        exps = {}
+        z_turned = {}
+        r_turned = {}
+        r_psum = {}
+        r_last = {}
+        blocks = {}
+        pair_sum = {}
+        weights = {}
+        products = {}
+        results = {}
+        LAST = UNITS - 1
 
-        def scores(i, js):
-            vc, b, uh = i // 4, (i // 2) % 2, i % 2
-            qcols = slice((2 * b + uh) * P, (2 * b + uh + 1) * P)
-            if 0 in js:
-                banks[i] = []
-            for j in js:
-                if j in G_BANKS:
-                    bank = psum.tile([P, 4, P], F32, name="s0", tag="pj")
+        def scores(unit, which):
+            half, block = unit // 4, unit % 4
+            q_cols = slice(block * P, (block + 1) * P)
+            codes, scales = key_packed[half]
+            if 0 in which:
+                banks[unit] = []
+            for j in which:
+                if j == 0:
+                    bank = psum.tile([P, GROUP, P], F32, name="scores0", tag="short")
                 else:
-                    bank = psum.tile([P, 4, P], F32, name="sc", tag="sc", bufs=3)
-                for a in range(4):
-                    cols = slice((4 * j + a) * P, (4 * j + a + 1) * P)
+                    bank = psum.tile([P, GROUP, P], F32, name="scores", tag="scores", bufs=3)
+                for g in range(GROUP):
+                    cols = slice((j * GROUP + g) * P, (j * GROUP + g + 1) * P)
                     nc.tensor.matmul_mx(
-                        out=bank[:, a, :],
-                        lhsT=kc[vc][:, cols].bitcast(FP8X4),
-                        lhsT_scale=ks[vc][:, cols],
-                        rhs=qc[:, qcols].bitcast(FP8X4),
-                        rhs_scale=qs[:, qcols],
+                        out=bank[:, g, :],
+                        lhsT=codes[:, cols].bitcast(FP8X4),
+                        lhsT_scale=scales[:, cols],
+                        rhs=q_codes[:, q_cols].bitcast(FP8X4),
+                        rhs_scale=q_scales[:, q_cols],
                         start=True,
                         stop=True,
                     )
-                banks[i].append(bank)
+                banks[unit].append(bank)
 
-        def copy_banks(i):
-            cps[i] = {}
-            for j in G_BANKS:
-                cp = pair.tile([P, 4, P], F32, name="cp%d" % j, tag="cp%d" % j)
-                nc.scalar.copy(out=cp[:], in_=banks[i][j][:])
-                cps[i][j] = cp
+        def copy_bank0(unit):
+            bank0_copy[unit] = work.tile([P, GROUP, P], F32, name="bank0_copy", tag="bank0_copy")
+            nc.scalar.copy(out=bank0_copy[unit][:], in_=banks[unit][0][:])
 
-        mxs = {}
+        def maximum(unit):
+            exps[unit] = work.tile([P, NS, P], F32, name="exps", tag="exps", bufs=3)
+            four = work.tile([P, GROUP, P], F32, name="max_of_banks", tag="max_of_banks")
+            nc.vector.tensor_tensor(out=four[:], in0=banks[unit][1][:], in1=bank0_copy[unit][:], op=ALU.max)
+            nc.vector.tensor_tensor(out=four[:], in0=banks[unit][2][:], in1=four[:], op=ALU.max)
+            nc.vector.tensor_tensor(out=four[:], in0=banks[unit][3][:], in1=four[:], op=ALU.max)
+            two = work.tile([P, 2, P], F32, name="max_of_two", tag="max_of_two")
+            nc.vector.tensor_tensor(out=two[:], in0=four[:, 0:2, :], in1=four[:, 2:4, :], op=ALU.max)
+            maxima[unit] = work.tile([P, P], F32, name="maxima", tag="maxima")
+            nc.vector.tensor_tensor(out=maxima[unit][:], in0=two[:, 0, :], in1=two[:, 1, :], op=ALU.max)
 
-        def maximum(i):
-            e = pair.tile([P, NS, P], F32, name="e", tag="e", bufs=3)
-            es[i] = e
-            bk = banks[i]
-            cp = cps[i]
-            t4 = pair.tile([P, 4, P], F32, name="t4", tag="t4")
-            if len(G_BANKS) == 1:
-                nc.vector.tensor_tensor(out=t4[:], in0=bk[1][:], in1=cp[0][:], op=ALU.max)
-                nc.vector.tensor_tensor(out=t4[:], in0=bk[2][:], in1=t4[:], op=ALU.max)
-                nc.vector.tensor_tensor(out=t4[:], in0=bk[3][:], in1=t4[:], op=ALU.max)
-            else:
-                t4b = pair.tile([P, 4, P], F32, name="t4b", tag="t4b")
-                nc.vector.tensor_tensor(out=t4[:], in0=bk[2][:], in1=cp[0][:], op=ALU.max)
-                nc.vector.tensor_tensor(out=t4b[:], in0=bk[3][:], in1=cp[1][:], op=ALU.max)
-                nc.vector.tensor_tensor(out=t4[:], in0=t4[:], in1=t4b[:], op=ALU.max)
-            t2 = pair.tile([P, 2, P], F32, name="t2", tag="t2")
-            nc.vector.tensor_tensor(out=t2[:], in0=t4[:, 0:2, :], in1=t4[:, 2:4, :], op=ALU.max)
-            mx = pair.tile([P, P], F32, name="mx", tag="mx")
-            nc.vector.tensor_tensor(out=mx[:], in0=t2[:, 0, :], in1=t2[:, 1, :], op=ALU.max)
-            mxs[i] = mx
-
-        def subtract(i, on_gpsimd):
-            e = es[i]
-            bk = banks[i]
-            cp = cps[i]
-            mx_b = mxs[i][:].unsqueeze(1).to_broadcast([P, 4, P])
-            for j in G_BANKS if on_gpsimd else ():
-                nc.gpsimd.tensor_tensor(
-                    out=e[:, 4 * j : 4 * j + 4, :], in0=cp[j][:], in1=mx_b, op=ALU.subtract
-                )
-            for j in () if on_gpsimd else range(4):
-                if j not in G_BANKS:
-                    nc.vector.tensor_tensor(
-                        out=e[:, 4 * j : 4 * j + 4, :], in0=bk[j][:], in1=mx_b, op=ALU.subtract
-                    )
-
-        def exponentials(i):
-            e = es[i]
-            for j in BANK_ORDER:
-                nc.scalar.activation(
-                    out=e[:, 4 * j : 4 * j + 4, :],
-                    in_=e[:, 4 * j : 4 * j + 4, :],
-                    func=ACT.Exp,
-                    scale=inv_sqrt,
-                )
-
-        def sum_over_images(i):
-            e = es[i]
-            zt = psum.tile([P, P], F32, name="zt", tag="z", bufs=1)
-            order = [4 * j + a for j in BANK_ORDER for a in range(4)]
-            for pos in range(NS):
-                nc.tensor.matmul(
-                    out=zt[:],
-                    lhsT=e[:, order[pos], :],
-                    rhs=ident[:],
-                    is_transpose=True,
-                    start=(pos == 0),
-                    stop=(pos == NS - 1),
-                )
-            zts[i] = zt
-
-        def reciprocal(i):
-            rt = pair.tile([P, P], F32, name="rt", tag="rt")
-            nc.vector.reciprocal(out=rt[:], in_=zts[i][:])
-            rts[i] = rt
-
-        rbs = {}
-
-        def reciprocal_back(i):
-            rp = psum.tile([P, P], F32, name="rp", tag="rp", bufs=1)
-            nc.tensor.transpose(rp[:], rts[i][:], ident[:])
-            rs[i] = rp
-            if G_MULT and i < G_MULT_UNITS:
-                rb = pair.tile([P, 64], F32, name="rb", tag="rb")
-                nc.scalar.copy(out=rb[:], in_=rp[:, 64:128])
-                rbs[i] = rb
-
-        def multiply(i, h):
-            if h == 0:
-                atts[i] = pair.tile([P, 16, NS, 8], F32, name="att", tag="att")
-            on_g = h in G_MULT and i < G_MULT_UNITS
-            eng = nc.gpsimd if on_g else nc.vector
-            us = slice(64 * h, 64 * h + 64)
-            eng.tensor_tensor(
-                out=atts[i][:, 8 * h : 8 * h + 8, :, :],
-                in0=es[i][:, :, us].rearrange("p n (g j) -> p g n j", j=8),
-                in1=(rbs[i][:] if on_g else rs[i][:, us])
-                .rearrange("p (g j) -> p g j", j=8)
-                .unsqueeze(2)
-                .to_broadcast([P, 8, NS, 8]),
-                op=ALU.mult,
+        def subtract(engine, unit, j, source):
+            engine.tensor_tensor(
+                out=exps[unit][:, j * GROUP : (j + 1) * GROUP, :],
+                in0=source[:],
+                in1=maxima[unit][:].unsqueeze(1).to_broadcast([P, GROUP, P]),
+                op=ALU.subtract,
             )
 
-        def add_blocks(i, h):
-            k, uh = i // 2, i % 2
-            if uh == 0 and h == 0:
-                p1s[k] = psum.tile([P, P], F32, name="p1", tag="acc", bufs=1)
-            for g in range(8 * h, 8 * h + 8):
-                nc.tensor.matmul(
-                    out=p1s[k][:],
-                    lhsT=atts[i][:, g, :, :].rearrange("p n j -> p (n j)"),
-                    rhs=ident[:],
-                    is_transpose=True,
-                    start=(uh == 0 and g == 0),
-                    stop=(uh == 1 and g == 15),
-                )
+        def exponentials(unit):
+            for j in range(4):
+                part = exps[unit][:, j * GROUP : (j + 1) * GROUP, :]
+                nc.scalar.activation(out=part, in_=part, func=ACT.Exp, scale=inv_sqrt)
 
-        ssums = {}
-
-        def sums_of_pair(k):
-            p1 = pair.tile([P, P], F32, name="p1s", tag="p1s")
-            nc.scalar.copy(out=p1[:], in_=p1s[k][:])
-            sp = psum.tile([P, NS], F32, name="sp", tag="pj")
-            nc.tensor.matmul(out=sp[:], lhsT=p1[:], rhs=sel[:], start=True, stop=True)
-            ssum = pair.tile([P, NS], F32, name="ssum", tag="ssum")
-            nc.scalar.copy(out=ssum[:], in_=sp[:])
-            ssums[k] = ssum
-
-        def products(k, half, on_vector):
-            vc = k // 2
-            ssum = ssums[k]
-            if half == 0:
-                prods[k] = pair.tile([P, NS, P], F32, name="prod", tag="prod")
-            prod = prods[k]
-            ns = slice(8 * half, 8 * half + 8)
-            if on_vector:
-                for n in range(8 * half, 8 * half + 8):
-                    nc.vector.tensor_scalar(
-                        out=prod[:, n, :],
-                        in0=vt[vc][:, n, :],
-                        scalar1=ssum[:, n : n + 1],
-                        scalar2=None,
-                        op0=ALU.mult,
-                    )
-            else:
-                ng_ = 8 - S_PROD
-                ns = slice(8 * half, 8 * half + ng_)
-                nc.gpsimd.tensor_tensor(
-                    out=prod[:, ns, :],
-                    in0=vt[vc][:, ns, :],
-                    in1=ssum[:, ns].unsqueeze(2).to_broadcast([P, ng_, P]),
-                    op=ALU.mult,
-                )
-                for n in range(8 * half + ng_, 8 * half + 8):
-                    nc.scalar.activation(
-                        out=prod[:, n, :], in_=vt[vc][:, n, :], func=ACT.Copy, scale=ssum[:, n : n + 1]
-                    )
-
-        def finish(k):
-            vc, b = k // 2, k % 2
-            res = psum.tile([P, P], F32, name="res", tag="pj")
+        def sum_over_images(unit):
+            z_turned[unit] = psum.tile([P, P], F32, name="z_turned", tag="zsum", bufs=1)
             for n in range(NS):
                 nc.tensor.matmul(
-                    out=res[:],
-                    lhsT=prods[k][:, n, :],
+                    out=z_turned[unit][:],
+                    lhsT=exps[unit][:, n, :],
                     rhs=ident[:],
                     is_transpose=True,
                     start=(n == 0),
                     stop=(n == NS - 1),
                 )
-            ot = pair.tile([P, P], F32, name="ot", tag="ot")
-            nc.scalar.copy(out=ot[:], in_=res[:])
-            nc.sync.dma_start(out=out[b, :, vc * P : (vc + 1) * P], in_=ot[:])
 
-        late = {}
-        EARLY = tuple(range(0, max(G_BANKS) + 1))
-        REST = tuple(range(max(G_BANKS) + 1, 4))
-        scores(0, EARLY)
-        copy_banks(0)
-        scores(0, REST)
-        for i in range(11):
-            if i + 1 < 8:
-                scores(i + 1, EARLY)
-                copy_banks(i + 1)
-            if i >= 4 and i % 2 == 0:
-                sums_of_pair((i - 4) // 2)
-            if i >= 6 and i % 2 == 0:
-                finish((i - 6) // 2)
-            if i <= 1:
-                for g in (2 * i, 2 * i + 1):
-                    late[g] = project_keys(1, 4 * g, 4, "pj", False)
-            if 3 <= i < 7:
-                for g in (0, 1):
-                    values((i - 3) // 2, 2 * ((i - 3) % 2) + g)
-            if i < 8:
-                maximum(i)
-                subtract(i, True)
-                subtract(i, False)
-            if i + 1 < 8:
-                scores(i + 1, REST)
-            if i < 8:
-                exponentials(i)
-            if i == 0:
-                quantise_support(1, 8, 4)
-                quantise_support(1, 12, 4)
-            if 2 <= i < 10:
-                multiply(i - 2, 0)
-                multiply(i - 2, 1)
-                add_blocks(i - 2, 0)
-                add_blocks(i - 2, 1)
-            if 1 <= i <= 8:
-                reciprocal(i - 1)
-                reciprocal_back(i - 1)
-            if i < 8:
-                sum_over_images(i)
-            if i <= 1:
-                for g in (2 * i, 2 * i + 1):
-                    quantise_keys(1, 4 * g, 4, late[g])
-            if 4 <= i < 10:
-                products((i - 4) // 2, i % 2, False)
-        products(3, 0, True)
-        products(3, 1, True)
-        finish(3)
+        def reciprocal(unit):
+            r_turned[unit] = work.tile([P, P], F32, name="r_turned", tag="r_turned")
+            nc.vector.reciprocal(out=r_turned[unit][:], in_=z_turned[unit][:])
+
+        def reciprocal_back(unit):
+            r_psum[unit] = psum.tile([P, P], F32, name="r_psum", tag="recip", bufs=1)
+            nc.tensor.transpose(r_psum[unit][:], r_turned[unit][:], ident[:])
+            if unit != LAST:
+                r_last[unit] = work.tile([P, P // 2], F32, name="r_last", tag="r_last")
+                nc.scalar.copy(out=r_last[unit][:], in_=r_psum[unit][:, P // 2 : P])
+
+        def multiply(unit, part):
+            if part == 0:
+                blocks[unit] = work.tile([P, P // TAIL, NS, TAIL], F32, name="blocks", tag="blocks")
+            us = slice(part * P // 2, (part + 1) * P // 2)
+            on_gpsimd = part == 1 and unit != LAST
+            engine = nc.gpsimd if on_gpsimd else nc.vector
+            r = r_last[unit][:] if on_gpsimd else r_psum[unit][:, us]
+            engine.tensor_tensor(
+                out=blocks[unit][:, part * 8 : (part + 1) * 8, :, :],
+                in0=exps[unit][:, :, us].rearrange("p n (g j) -> p g n j", j=TAIL),
+                in1=r.rearrange("p (g j) -> p g j", j=TAIL).unsqueeze(2).to_broadcast([P, 8, NS, TAIL]),
+                op=ALU.mult,
+            )
+
+        def add_blocks(unit):
+            pair, second = unit // 2, unit % 2
+            if second == 0:
+                pair_sum[pair] = psum.tile([P, P], F32, name="pair_sum", tag="pairsum", bufs=1)
+            for g in range(P // TAIL):
+                nc.tensor.matmul(
+                    out=pair_sum[pair][:],
+                    lhsT=blocks[unit][:, g, :, :].rearrange("p n j -> p (n j)"),
+                    rhs=ident[:],
+                    is_transpose=True,
+                    start=(second == 0 and g == 0),
+                    stop=(second == 1 and g == P // TAIL - 1),
+                )
+
+        def weights_of_pair(pair):
+            summed = work.tile([P, P], F32, name="pair_sum_sb", tag="pair_sum_sb")
+            nc.scalar.copy(out=summed[:], in_=pair_sum[pair][:])
+            turned_sum = psum.tile([P, NS], F32, name="weights_psum", tag="short")
+            nc.tensor.matmul(out=turned_sum[:], lhsT=summed[:], rhs=same_image[:], start=True, stop=True)
+            weights[pair] = work.tile([P, NS], F32, name="weights", tag="weights")
+            nc.scalar.copy(out=weights[pair][:], in_=turned_sum[:])
+
+        def weigh_values(pair, part):
+            if part == 0:
+                products[pair] = work.tile([P, NS, P], F32, name="products", tag="products")
+            val = val_t[pair // 2]
+            if pair == PAIRS - 1:
+                for n in range(part * 8, (part + 1) * 8):
+                    nc.vector.tensor_scalar(
+                        out=products[pair][:, n, :],
+                        in0=val[:, n, :],
+                        scalar1=weights[pair][:, n : n + 1],
+                        scalar2=None,
+                        op0=ALU.mult,
+                    )
+            else:
+                ns = slice(part * 8, (part + 1) * 8)
+                nc.gpsimd.tensor_tensor(
+                    out=products[pair][:, ns, :],
+                    in0=val[:, ns, :],
+                    in1=weights[pair][:, ns].unsqueeze(2).to_broadcast([P, 8, P]),
+                    op=ALU.mult,
+                )
+
+        def add_products(pair):
+            results[pair] = psum.tile([P, P], F32, name="result", tag="short")
+            for n in range(NS):
+                nc.tensor.matmul(
+                    out=results[pair][:],
+                    lhsT=products[pair][:, n, :],
+                    rhs=ident[:],
+                    is_transpose=True,
+                    start=(n == 0),
+                    stop=(n == NS - 1),
+                )
+
+        def store(pair):
+            half, b = pair // 2, pair % 2
+            result_sb = work.tile([P, P], F32, name="result_sb", tag="result_sb")
+            nc.scalar.copy(out=result_sb[:], in_=results[pair][:])
+            nc.sync.dma_start(out=out[b, :, half * P : (half + 1) * P], in_=result_sb[:])
+
+        scores(0, (0,))
+        copy_bank0(0)
+        scores(0, (1, 2, 3))
+        late_keys = {}
+        for slot in range(UNITS + 3):
+            if slot + 1 < UNITS:
+                scores(slot + 1, (0,))
+                copy_bank0(slot + 1)
+            if pair_due(slot, 4) is not None:
+                weights_of_pair(pair_due(slot, 4))
+            if slot < 2:
+                for group in (2 * slot, 2 * slot + 1):
+                    late_keys[group] = project_keys(1, group, "short")
+            if 3 <= slot < 7:
+                for group in (2 * ((slot - 3) % 2), 2 * ((slot - 3) % 2) + 1):
+                    values((slot - 3) // 2, group)
+            if slot < UNITS:
+                maximum(slot)
+                subtract(nc.gpsimd, slot, 0, bank0_copy[slot])
+                for j in (1, 2, 3):
+                    subtract(nc.vector, slot, j, banks[slot][j])
+            if slot + 1 < UNITS:
+                scores(slot + 1, (1, 2, 3))
+            if slot < UNITS:
+                exponentials(slot)
+            if slot == 0:
+                quantise_support(1, 2)
+                quantise_support(1, 3)
+            if 0 <= slot - 2 < UNITS:
+                multiply(slot - 2, 0)
+                multiply(slot - 2, 1)
+                add_blocks(slot - 2)
+            if 0 <= slot - 1 < UNITS:
+                reciprocal(slot - 1)
+                reciprocal_back(slot - 1)
+            if slot < UNITS:
+                sum_over_images(slot)
+            if slot < 2:
+                for group in (2 * slot, 2 * slot + 1):
+                    quantise_keys(1, group, late_keys[group])
+            if 0 <= slot - 4 < 2 * (PAIRS - 1):
+                weigh_values((slot - 4) // 2, (slot - 4) % 2)
+            if pair_due(slot, 7) is not None:
+                store(pair_due(slot, 7))
+            if pair_due(slot, 6) is not None:
+                add_products(pair_due(slot, 6))
+        weigh_values(PAIRS - 1, 0)
+        weigh_values(PAIRS - 1, 1)
+        store(PAIRS - 2)
+        add_products(PAIRS - 1)
+        store(PAIRS - 1)

@@ -22,6 +22,7 @@ GROUPS = NS // GROUP
 UNITS = 8
 PAIRS = UNITS // 2
 TAIL = 8
+STRIPS = P // TAIL
 FLOPS = 2 * 512 * 512 * 256 * (NB + NS) + 2 * 128 * 512 * 256 * NS + 2 * 512 * 256 * 256 * NB * NS
 
 
@@ -73,23 +74,23 @@ def tile_crossattention_pa_kernel(tc, query, support, Wk, Wv, out):
         wk_words = wk_sb[:].bitcast(F32).rearrange("p (m w u) -> p m w u", m=PACK, u=2)
         wk_grouped = keep.tile([P, PACK * 512], BF16, name="wk_grouped", align_bytes=64)
         wk_grouped_words = wk_grouped[:].bitcast(F32).rearrange("p (m c u) -> p m c u", m=PACK, u=2)
-        turned = []
+        wk_turned = []
         for first in (0, 2):
             bank = psum.tile([P, 2, 2, P], F32, name="wk_turned", tag="short")
             for m in range(2):
                 for u in range(2):
                     nc.tensor.transpose(bank[:, m, u, :], wk_words[:, first + m, :, u], ident[:])
-            turned.append(bank)
+            wk_turned.append(bank)
         for first in (0, 2):
             nc.scalar.copy(
                 out=wk_grouped_words[:, first : first + 2, :, :],
-                in_=turned[first // 2][:].rearrange("p m u c -> p m c u"),
+                in_=wk_turned[first // 2][:].rearrange("p m u c -> p m c u"),
             )
         wk_codes, wk_scales = packed("wk", 512)
 
-        def project(codes, scales, block, tag):
+        def project(codes, scales, piece, tag):
             bank = psum.tile([P, PACK, P], F32, name="projected", tag=tag, bufs=(3 if tag == "scores" else 2))
-            cols = slice(block * P, (block + 1) * P)
+            cols = slice(piece * P, (piece + 1) * P)
             for m in range(PACK):
                 chunk = slice(m * P, (m + 1) * P)
                 nc.tensor.matmul_mx(
@@ -140,9 +141,9 @@ def tile_crossattention_pa_kernel(tc, query, support, Wk, Wv, out):
         qf_codes, qf_scales = packed("qf", NB * 256)
         quantise(qf_codes[:], qf_scales[:], qf_grouped[:])
         q_grouped = keep.tile([P, NB * 256 * PACK], BF16, name="q_grouped", align_bytes=64)
-        q_by_block = q_grouped[:].rearrange("p (g w m) -> p g w m", g=2 * NB, m=PACK)
-        for block in range(2 * NB):
-            round_and_group(q_by_block[:, block], project(qf_codes, qf_scales, block, "scores"))
+        q_by_piece = q_grouped[:].rearrange("p (g w m) -> p g w m", g=2 * NB, m=PACK)
+        for piece in range(2 * NB):
+            round_and_group(q_by_piece[:, piece], project(qf_codes, qf_scales, piece, "scores"))
         q_codes, q_scales = packed("q", NB * 256)
 
         wv_words = wv_sb[:].bitcast(F32).rearrange("p (w u) -> p w u", u=2)
@@ -195,7 +196,7 @@ def tile_crossattention_pa_kernel(tc, query, support, Wk, Wv, out):
         r_turned = {}
         r_psum = {}
         r_last = {}
-        blocks = {}
+        strips = {}
         pair_sum = {}
         weights = {}
         products = {}
@@ -203,8 +204,8 @@ def tile_crossattention_pa_kernel(tc, query, support, Wk, Wv, out):
         LAST = UNITS - 1
 
         def scores(unit, which):
-            half, block = unit // 4, unit % 4
-            q_cols = slice(block * P, (block + 1) * P)
+            half, piece = unit // 4, unit % 4
+            q_cols = slice(piece * P, (piece + 1) * P)
             codes, scales = key_packed[half]
             if 0 in which:
                 banks[unit] = []
@@ -250,9 +251,9 @@ def tile_crossattention_pa_kernel(tc, query, support, Wk, Wv, out):
             )
 
         def exponentials(unit):
-            for j in range(4):
-                part = exps[unit][:, j * GROUP : (j + 1) * GROUP, :]
-                nc.scalar.activation(out=part, in_=part, func=ACT.Exp, scale=inv_sqrt)
+            for j in range(GROUPS):
+                four_images = exps[unit][:, j * GROUP : (j + 1) * GROUP, :]
+                nc.scalar.activation(out=four_images, in_=four_images, func=ACT.Exp, scale=inv_sqrt)
 
         def sum_over_images(unit):
             z_turned[unit] = psum.tile([P, P], F32, name="z_turned", tag="zsum", bufs=1)
@@ -279,30 +280,30 @@ def tile_crossattention_pa_kernel(tc, query, support, Wk, Wv, out):
 
         def multiply(unit, part):
             if part == 0:
-                blocks[unit] = work.tile([P, P // TAIL, NS, TAIL], F32, name="blocks", tag="blocks")
+                strips[unit] = work.tile([P, STRIPS, NS, TAIL], F32, name="strips", tag="strips")
             us = slice(part * P // 2, (part + 1) * P // 2)
             on_gpsimd = part == 1 and unit != LAST
             engine = nc.gpsimd if on_gpsimd else nc.vector
             r = r_last[unit][:] if on_gpsimd else r_psum[unit][:, us]
             engine.tensor_tensor(
-                out=blocks[unit][:, part * 8 : (part + 1) * 8, :, :],
+                out=strips[unit][:, part * STRIPS // 2 : (part + 1) * STRIPS // 2, :, :],
                 in0=exps[unit][:, :, us].rearrange("p n (g j) -> p g n j", j=TAIL),
-                in1=r.rearrange("p (g j) -> p g j", j=TAIL).unsqueeze(2).to_broadcast([P, 8, NS, TAIL]),
+                in1=r.rearrange("p (g j) -> p g j", j=TAIL).unsqueeze(2).to_broadcast([P, STRIPS // 2, NS, TAIL]),
                 op=ALU.mult,
             )
 
-        def add_blocks(unit):
+        def add_strips(unit):
             pair, second = unit // 2, unit % 2
             if second == 0:
                 pair_sum[pair] = psum.tile([P, P], F32, name="pair_sum", tag="pairsum", bufs=1)
-            for g in range(P // TAIL):
+            for g in range(STRIPS):
                 nc.tensor.matmul(
                     out=pair_sum[pair][:],
-                    lhsT=blocks[unit][:, g, :, :].rearrange("p n j -> p (n j)"),
+                    lhsT=strips[unit][:, g, :, :].rearrange("p n j -> p (n j)"),
                     rhs=ident[:],
                     is_transpose=True,
                     start=(second == 0 and g == 0),
-                    stop=(second == 1 and g == P // TAIL - 1),
+                    stop=(second == 1 and g == STRIPS - 1),
                 )
 
         def weights_of_pair(pair):
@@ -313,38 +314,51 @@ def tile_crossattention_pa_kernel(tc, query, support, Wk, Wv, out):
             weights[pair] = work.tile([P, NS], F32, name="weights", tag="weights")
             nc.scalar.copy(out=weights[pair][:], in_=turned_sum[:])
 
-        def weigh_values(pair, part):
-            if part == 0:
-                products[pair] = work.tile([P, NS, P], F32, name="products", tag="products")
+        EIGHT = NS // 2
+
+        def weigh_values(pair):
+            products[pair] = work.tile([P, NS, P], F32, name="products", tag="products")
             val = val_t[pair // 2]
-            if pair == PAIRS - 1:
-                for n in range(part * 8, (part + 1) * 8):
-                    nc.vector.tensor_scalar(
-                        out=products[pair][:, n, :],
-                        in0=val[:, n, :],
-                        scalar1=weights[pair][:, n : n + 1],
-                        scalar2=None,
-                        op0=ALU.mult,
-                    )
-            else:
-                ns = slice(part * 8, (part + 1) * 8)
-                nc.gpsimd.tensor_tensor(
-                    out=products[pair][:, ns, :],
-                    in0=val[:, ns, :],
-                    in1=weights[pair][:, ns].unsqueeze(2).to_broadcast([P, 8, P]),
-                    op=ALU.mult,
+            nc.gpsimd.tensor_tensor(
+                out=products[pair][:, 0:EIGHT, :],
+                in0=val[:, 0:EIGHT, :],
+                in1=weights[pair][:, 0:EIGHT].unsqueeze(2).to_broadcast([P, EIGHT, P]),
+                op=ALU.mult,
+            )
+            for n in range(EIGHT, NS):
+                nc.scalar.activation(
+                    out=products[pair][:, n, :], in_=val[:, n, :], func=ACT.Copy, scale=weights[pair][:, n : n + 1]
                 )
 
-        def add_products(pair):
-            results[pair] = psum.tile([P, P], F32, name="result", tag="short")
+        def fold_products(pair):
+            nc.gpsimd.tensor_tensor(
+                out=products[pair][:, 0:EIGHT, :],
+                in0=products[pair][:, 0:EIGHT, :],
+                in1=products[pair][:, EIGHT:NS, :],
+                op=ALU.add,
+            )
+
+        def weigh_values_on_vector(pair):
+            products[pair] = work.tile([P, NS, P], F32, name="products", tag="products")
             for n in range(NS):
+                nc.vector.tensor_scalar(
+                    out=products[pair][:, n, :],
+                    in0=val_t[pair // 2][:, n, :],
+                    scalar1=weights[pair][:, n : n + 1],
+                    scalar2=None,
+                    op0=ALU.mult,
+                )
+
+        def add_products(pair, count):
+            results[pair] = psum.tile([P, P], F32, name="result", tag="short")
+            for n in range(count):
                 nc.tensor.matmul(
                     out=results[pair][:],
                     lhsT=products[pair][:, n, :],
                     rhs=ident[:],
                     is_transpose=True,
                     start=(n == 0),
-                    stop=(n == NS - 1),
+                    stop=(n == count - 1),
                 )
 
         def store(pair):
@@ -366,9 +380,9 @@ def tile_crossattention_pa_kernel(tc, query, support, Wk, Wv, out):
             if slot < 2:
                 for group in (2 * slot, 2 * slot + 1):
                     late_keys[group] = project_keys(1, group, "short")
-            if 3 <= slot < 7:
-                for group in (2 * ((slot - 3) % 2), 2 * ((slot - 3) % 2) + 1):
-                    values((slot - 3) // 2, group)
+            if 2 <= slot < 6:
+                for group in (2 * (slot % 2), 2 * (slot % 2) + 1):
+                    values((slot - 2) // 2, group)
             if slot < UNITS:
                 maximum(slot)
                 subtract(nc.gpsimd, slot, 0, bank0_copy[slot])
@@ -384,7 +398,7 @@ def tile_crossattention_pa_kernel(tc, query, support, Wk, Wv, out):
             if 0 <= slot - 2 < UNITS:
                 multiply(slot - 2, 0)
                 multiply(slot - 2, 1)
-                add_blocks(slot - 2)
+                add_strips(slot - 2)
             if 0 <= slot - 1 < UNITS:
                 reciprocal(slot - 1)
                 reciprocal_back(slot - 1)
@@ -393,14 +407,15 @@ def tile_crossattention_pa_kernel(tc, query, support, Wk, Wv, out):
             if slot < 2:
                 for group in (2 * slot, 2 * slot + 1):
                     quantise_keys(1, group, late_keys[group])
-            if 0 <= slot - 4 < 2 * (PAIRS - 1):
-                weigh_values((slot - 4) // 2, (slot - 4) % 2)
+            if pair_due(slot, 4) is not None and pair_due(slot, 4) != PAIRS - 1:
+                weigh_values(pair_due(slot, 4))
+            if pair_due(slot, 5) is not None:
+                fold_products(pair_due(slot, 5))
             if pair_due(slot, 7) is not None:
                 store(pair_due(slot, 7))
             if pair_due(slot, 6) is not None:
-                add_products(pair_due(slot, 6))
-        weigh_values(PAIRS - 1, 0)
-        weigh_values(PAIRS - 1, 1)
+                add_products(pair_due(slot, 6), EIGHT)
+        weigh_values_on_vector(PAIRS - 1)
         store(PAIRS - 2)
-        add_products(PAIRS - 1)
+        add_products(PAIRS - 1, NS)
         store(PAIRS - 1)

@@ -201,7 +201,6 @@ def tile_crossattention_pa_kernel(tc, query, support, Wk, Wv, out):
         weights = {}
         products = {}
         results = {}
-        LAST = UNITS - 1
 
         def scores(unit, which):
             half, piece = unit // 4, unit % 4
@@ -231,16 +230,20 @@ def tile_crossattention_pa_kernel(tc, query, support, Wk, Wv, out):
             bank0_copy[unit] = work.tile([P, GROUP, P], F32, name="bank0_copy", tag="bank0_copy")
             nc.scalar.copy(out=bank0_copy[unit][:], in_=banks[unit][0][:])
 
-        def maximum(unit):
-            exps[unit] = work.tile([P, NS, P], F32, name="exps", tag="exps", bufs=3)
-            four = work.tile([P, GROUP, P], F32, name="max_of_banks", tag="max_of_banks")
-            nc.vector.tensor_tensor(out=four[:], in0=banks[unit][1][:], in1=bank0_copy[unit][:], op=ALU.max)
-            nc.vector.tensor_tensor(out=four[:], in0=banks[unit][2][:], in1=four[:], op=ALU.max)
-            nc.vector.tensor_tensor(out=four[:], in0=banks[unit][3][:], in1=four[:], op=ALU.max)
-            two = work.tile([P, 2, P], F32, name="max_of_two", tag="max_of_two")
-            nc.vector.tensor_tensor(out=two[:], in0=four[:, 0:2, :], in1=four[:, 2:4, :], op=ALU.max)
+        four = {}
+
+        def maximum_of_bank(unit, j):
+            if j == 1:
+                exps[unit] = work.tile([P, NS, P], F32, name="exps", tag="exps", bufs=3)
+                four[unit] = work.tile([P, GROUP, P], F32, name="max_of_banks", tag="max_of_banks")
+            other = bank0_copy[unit] if j == 1 else four[unit]
+            nc.vector.tensor_tensor(out=four[unit][:], in0=banks[unit][j][:], in1=other[:], op=ALU.max)
+
+        def maximum_of_four(unit):
             maxima[unit] = work.tile([P, P], F32, name="maxima", tag="maxima")
-            nc.vector.tensor_tensor(out=maxima[unit][:], in0=two[:, 0, :], in1=two[:, 1, :], op=ALU.max)
+            nc.vector.tensor_reduce(
+                out=maxima[unit][:], in_=four[unit][:].rearrange("p n u -> p u n"), axis=AX.X, op=ALU.max
+            )
 
         def subtract(engine, unit, j, source):
             engine.tensor_tensor(
@@ -250,21 +253,21 @@ def tile_crossattention_pa_kernel(tc, query, support, Wk, Wv, out):
                 op=ALU.subtract,
             )
 
-        def exponentials(unit):
-            for j in range(GROUPS):
-                four_images = exps[unit][:, j * GROUP : (j + 1) * GROUP, :]
-                nc.scalar.activation(out=four_images, in_=four_images, func=ACT.Exp, scale=inv_sqrt)
+        def exponentials(unit, j):
+            four_images = exps[unit][:, j * GROUP : (j + 1) * GROUP, :]
+            nc.scalar.activation(out=four_images, in_=four_images, func=ACT.Exp, scale=inv_sqrt)
 
         def sum_over_images(unit):
             z_turned[unit] = psum.tile([P, P], F32, name="z_turned", tag="zsum", bufs=1)
-            for n in range(NS):
+            order = [j * GROUP + g for j in (1, 2, 3, 0) for g in range(GROUP)]
+            for n in order:
                 nc.tensor.matmul(
                     out=z_turned[unit][:],
                     lhsT=exps[unit][:, n, :],
                     rhs=ident[:],
                     is_transpose=True,
-                    start=(n == 0),
-                    stop=(n == NS - 1),
+                    start=(n == order[0]),
+                    stop=(n == order[-1]),
                 )
 
         def reciprocal(unit):
@@ -274,73 +277,80 @@ def tile_crossattention_pa_kernel(tc, query, support, Wk, Wv, out):
         def reciprocal_back(unit):
             r_psum[unit] = psum.tile([P, P], F32, name="r_psum", tag="recip", bufs=1)
             nc.tensor.transpose(r_psum[unit][:], r_turned[unit][:], ident[:])
-            if unit != LAST:
-                r_last[unit] = work.tile([P, P // 2], F32, name="r_last", tag="r_last")
-                nc.scalar.copy(out=r_last[unit][:], in_=r_psum[unit][:, P // 2 : P])
 
-        def multiply(unit, part):
-            if part == 0:
+        def reciprocal_out(unit):
+            r_last[unit] = work.tile([P, P], F32, name="r_last", tag="r_last")
+            nc.scalar.copy(out=r_last[unit][:], in_=r_psum[unit][:])
+
+        def multiply(engine, unit, first, count):
+            if unit not in strips:
                 strips[unit] = work.tile([P, STRIPS, NS, TAIL], F32, name="strips", tag="strips")
-            us = slice(part * P // 2, (part + 1) * P // 2)
-            on_gpsimd = part == 1 and unit != LAST
-            engine = nc.gpsimd if on_gpsimd else nc.vector
-            r = r_last[unit][:] if on_gpsimd else r_psum[unit][:, us]
+            us = slice(first * TAIL, (first + count) * TAIL)
+            r = r_psum[unit][:, us] if engine is nc.vector else r_last[unit][:, us]
             engine.tensor_tensor(
-                out=strips[unit][:, part * STRIPS // 2 : (part + 1) * STRIPS // 2, :, :],
+                out=strips[unit][:, first : first + count, :, :],
                 in0=exps[unit][:, :, us].rearrange("p n (g j) -> p g n j", j=TAIL),
-                in1=r.rearrange("p (g j) -> p g j", j=TAIL).unsqueeze(2).to_broadcast([P, STRIPS // 2, NS, TAIL]),
+                in1=r.rearrange("p (g j) -> p g j", j=TAIL).unsqueeze(2).to_broadcast([P, count, NS, TAIL]),
                 op=ALU.mult,
             )
 
-        def add_strips(unit):
-            pair, second = unit // 2, unit % 2
-            if second == 0:
+        added = {}
+
+        def add_strips(unit, first, count):
+            pair = unit // 2
+            if pair not in pair_sum:
                 pair_sum[pair] = psum.tile([P, P], F32, name="pair_sum", tag="pairsum", bufs=1)
-            for g in range(STRIPS):
+                added[pair] = 0
+            for g in range(first, first + count):
                 nc.tensor.matmul(
                     out=pair_sum[pair][:],
                     lhsT=strips[unit][:, g, :, :].rearrange("p n j -> p (n j)"),
                     rhs=ident[:],
                     is_transpose=True,
-                    start=(second == 0 and g == 0),
-                    stop=(second == 1 and g == STRIPS - 1),
+                    start=(added[pair] == 0),
+                    stop=(added[pair] == 2 * STRIPS - 1),
+                )
+                added[pair] += 1
+
+        summed = {}
+        turned_sum = {}
+
+        def pair_sum_copy(pair):
+            summed[pair] = work.tile([P, P], F32, name="pair_sum_sb", tag="pair_sum_sb")
+            nc.scalar.copy(out=summed[pair][:], in_=pair_sum[pair][:])
+
+        def pair_sum_turn(pair):
+            turned_sum[pair] = psum.tile([P, NS], F32, name="weights_psum", tag="short")
+            nc.tensor.matmul(out=turned_sum[pair][:], lhsT=summed[pair][:], rhs=same_image[:], start=True, stop=True)
+
+        def weights_out(pair):
+            weights[pair] = work.tile([P, NS], F32, name="weights", tag="weights")
+            nc.scalar.copy(out=weights[pair][:], in_=turned_sum[pair][:])
+
+        def weigh_on_scalar(pair, images):
+            if pair not in products:
+                products[pair] = work.tile([P, NS, P], F32, name="products", tag="products")
+            for n in images:
+                nc.scalar.activation(
+                    out=products[pair][:, n, :],
+                    in_=val_t[pair // 2][:, n, :],
+                    func=ACT.Copy,
+                    scale=weights[pair][:, n : n + 1],
                 )
 
-        def weights_of_pair(pair):
-            summed = work.tile([P, P], F32, name="pair_sum_sb", tag="pair_sum_sb")
-            nc.scalar.copy(out=summed[:], in_=pair_sum[pair][:])
-            turned_sum = psum.tile([P, NS], F32, name="weights_psum", tag="short")
-            nc.tensor.matmul(out=turned_sum[:], lhsT=summed[:], rhs=same_image[:], start=True, stop=True)
-            weights[pair] = work.tile([P, NS], F32, name="weights", tag="weights")
-            nc.scalar.copy(out=weights[pair][:], in_=turned_sum[:])
-
-        EIGHT = NS // 2
-
-        def weigh_values(pair):
+        def weigh_on_gpsimd(pair, count):
             products[pair] = work.tile([P, NS, P], F32, name="products", tag="products")
-            val = val_t[pair // 2]
             nc.gpsimd.tensor_tensor(
-                out=products[pair][:, 0:EIGHT, :],
-                in0=val[:, 0:EIGHT, :],
-                in1=weights[pair][:, 0:EIGHT].unsqueeze(2).to_broadcast([P, EIGHT, P]),
+                out=products[pair][:, 0:count, :],
+                in0=val_t[pair // 2][:, 0:count, :],
+                in1=weights[pair][:, 0:count].unsqueeze(2).to_broadcast([P, count, P]),
                 op=ALU.mult,
             )
-            for n in range(EIGHT, NS):
-                nc.scalar.activation(
-                    out=products[pair][:, n, :], in_=val[:, n, :], func=ACT.Copy, scale=weights[pair][:, n : n + 1]
-                )
 
-        def fold_products(pair):
-            nc.gpsimd.tensor_tensor(
-                out=products[pair][:, 0:EIGHT, :],
-                in0=products[pair][:, 0:EIGHT, :],
-                in1=products[pair][:, EIGHT:NS, :],
-                op=ALU.add,
-            )
-
-        def weigh_values_on_vector(pair):
-            products[pair] = work.tile([P, NS, P], F32, name="products", tag="products")
-            for n in range(NS):
+        def weigh_on_vector(pair, images):
+            if pair not in products:
+                products[pair] = work.tile([P, NS, P], F32, name="products", tag="products")
+            for n in images:
                 nc.vector.tensor_scalar(
                     out=products[pair][:, n, :],
                     in0=val_t[pair // 2][:, n, :],
@@ -349,16 +359,16 @@ def tile_crossattention_pa_kernel(tc, query, support, Wk, Wv, out):
                     op0=ALU.mult,
                 )
 
-        def add_products(pair, count):
+        def add_products(pair):
             results[pair] = psum.tile([P, P], F32, name="result", tag="short")
-            for n in range(count):
+            for n in range(NS):
                 nc.tensor.matmul(
                     out=results[pair][:],
                     lhsT=products[pair][:, n, :],
                     rhs=ident[:],
                     is_transpose=True,
                     start=(n == 0),
-                    stop=(n == count - 1),
+                    stop=(n == NS - 1),
                 )
 
         def store(pair):
@@ -370,52 +380,99 @@ def tile_crossattention_pa_kernel(tc, query, support, Wk, Wv, out):
         scores(0, (0,))
         copy_bank0(0)
         scores(0, (1, 2, 3))
-        late_keys = {}
-        for slot in range(UNITS + 3):
-            if slot + 1 < UNITS:
-                scores(slot + 1, (0,))
-                copy_bank0(slot + 1)
-            if pair_due(slot, 4) is not None:
-                weights_of_pair(pair_due(slot, 4))
-            if slot < 2:
-                for group in (2 * slot, 2 * slot + 1):
-                    late_keys[group] = project_keys(1, group, "short")
-            if 2 <= slot < 6:
-                for group in (2 * (slot % 2), 2 * (slot % 2) + 1):
-                    values((slot - 2) // 2, group)
-            if slot < UNITS:
-                maximum(slot)
-                subtract(nc.gpsimd, slot, 0, bank0_copy[slot])
+        late_keys = {0: project_keys(1, 0, "short")}
+        LAST = UNITS - 1
+        for slot in range(UNITS + 1):
+            unit, last, older = slot, slot - 1, slot - 2
+            live, live_last, live_older = unit < UNITS, 0 <= last < UNITS, 0 <= older < LAST - 1
+            pair = pair_due(slot, 4)
+            if live_last:
+                sum_over_images(last)
+            if unit + 1 < UNITS:
+                scores(unit + 1, (0,))
+                copy_bank0(unit + 1)
+            if pair is not None:
+                pair_sum_turn(pair)
+            if slot < 3:
+                late_keys[slot + 1] = project_keys(1, slot + 1, "short")
+            if live:
+                maximum_of_bank(unit, 1)
+            if live_older:
+                multiply(nc.gpsimd, older, 9, 7)
+                multiply(nc.vector, older, 0, 1)
+            if live:
+                maximum_of_bank(unit, 2)
+            if live_older:
+                multiply(nc.vector, older, 1, 1)
+                add_strips(older, 0, 9)
+            if live:
+                maximum_of_bank(unit, 3)
+                maximum_of_four(unit)
+                subtract(nc.gpsimd, unit, 0, bank0_copy[unit])
+            if live_last and slot < LAST:
+                reciprocal(last)
+                reciprocal_back(last)
+                reciprocal_out(last)
+            if pair is not None:
+                weights_out(pair)
+            if live:
                 for j in (1, 2, 3):
-                    subtract(nc.vector, slot, j, banks[slot][j])
-            if slot + 1 < UNITS:
-                scores(slot + 1, (1, 2, 3))
-            if slot < UNITS:
-                exponentials(slot)
-            if slot == 0:
-                quantise_support(1, 2)
-                quantise_support(1, 3)
-            if 0 <= slot - 2 < UNITS:
-                multiply(slot - 2, 0)
-                multiply(slot - 2, 1)
-                add_strips(slot - 2)
-            if 0 <= slot - 1 < UNITS:
-                reciprocal(slot - 1)
-                reciprocal_back(slot - 1)
-            if slot < UNITS:
-                sum_over_images(slot)
+                    subtract(nc.vector, unit, j, banks[unit][j])
+            if live_last and slot >= LAST:
+                reciprocal(last)
+            if live_older:
+                add_strips(older, 9, 7)
+            if unit + 1 < UNITS:
+                scores(unit + 1, (1, 2, 3))
+            if live_last and slot >= LAST:
+                reciprocal_back(last)
+            if live:
+                for j in (1, 2, 3, 0):
+                    exponentials(unit, j)
+            if slot == LAST:
+                reciprocal_out(last)
+            if live_last and slot < LAST:
+                multiply(nc.gpsimd, last, 2, 7)
+            if slot == LAST:
+                multiply(nc.vector, last, 0, 4)
+                multiply(nc.vector, last, 4, 4)
+                multiply(nc.gpsimd, last, 8, 4)
+                multiply(nc.gpsimd, last, 12, 4)
+            if pair_due(slot, 3) is not None:
+                pair_sum_copy(pair_due(slot, 3))
+            if slot in (2, 3):
+                values(0, 2 * slot - 4)
+                values(0, 2 * slot - 3)
+            if slot in (4, 5, 6):
+                values(1, slot - 4)
+            if slot == 6:
+                values(1, 3)
+            if slot in (4, 6):
+                weigh_on_scalar((slot - 4) // 2, range(0, NS // 2))
+            if slot in (5, 7):
+                weigh_on_scalar((slot - 5) // 2, range(NS // 2, NS))
+            if slot == LAST + 1:
+                for first in range(0, STRIPS, 4):
+                    multiply(nc.vector, LAST, first, 4)
+                weigh_on_gpsimd(2, 8)
+                weigh_on_scalar(2, range(8, NS))
+                add_strips(LAST - 1, 0, STRIPS)
+                add_strips(LAST, 0, STRIPS)
             if slot < 2:
-                for group in (2 * slot, 2 * slot + 1):
-                    quantise_keys(1, group, late_keys[group])
-            if pair_due(slot, 4) is not None and pair_due(slot, 4) != PAIRS - 1:
-                weigh_values(pair_due(slot, 4))
-            if pair_due(slot, 5) is not None:
-                fold_products(pair_due(slot, 5))
-            if pair_due(slot, 7) is not None:
-                store(pair_due(slot, 7))
-            if pair_due(slot, 6) is not None:
-                add_products(pair_due(slot, 6), EIGHT)
-        weigh_values_on_vector(PAIRS - 1)
-        store(PAIRS - 2)
-        add_products(PAIRS - 1, NS)
-        store(PAIRS - 1)
+                quantise_support(1, slot + 2)
+            if slot < 3:
+                quantise_keys(1, slot, late_keys[slot])
+            if slot == 2:
+                quantise_keys(1, 3, late_keys[3])
+            if slot in (6, 8):
+                add_products((slot - 6) // 2)
+                store((slot - 6) // 2)
+        pair_sum_copy(3)
+        pair_sum_turn(3)
+        weights_out(3)
+        weigh_on_vector(3, range(0, 11))
+        weigh_on_scalar(3, range(11, NS))
+        add_products(2)
+        add_products(3)
+        store(2)
+        store(3)

@@ -41,17 +41,23 @@ def tile_crossattention_pa_kernel(tc, query, support, Wk, Wv, out):
         ctx.enter_context(tc.manual_schedule())
 
         wk_sb = keep.tile([P, PACK * 512], BF16, name="wk_sb")
-        nc.sync.dma_start(out=wk_sb[:], in_=Wk.rearrange("(p m) d -> p (m d)", m=PACK))
+        for h in range(2):
+            nc.sync.dma_start(
+                out=wk_sb[:, h * 1024 : (h + 1) * 1024],
+                in_=Wk.rearrange("(p h m) d -> p h (m d)", h=2, m=2)[:, h, :],
+            )
         q_sb = keep.tile([P, NB, PACK * 256], BF16, name="q_sb")
-        nc.sync.dma_start(out=q_sb[:], in_=query.rearrange("b (p j) h w -> p b (j h w)", j=PACK))
+        for b in range(NB):
+            nc.sync.dma_start(out=q_sb[:, b, :], in_=query[b].rearrange("(p j) h w -> p (j h w)", j=PACK))
         wv_sb = keep.tile([P, 512], BF16, name="wv_sb")
-        nc.sync.dma_start(out=wv_sb[:], in_=Wv)
         sf_sb = keep.tile([P, NS, PACK * 256], BF16, name="sf_sb")
         for n in range(0, NS, 2):
             nc.sync.dma_start(
                 out=sf_sb[:, n : n + 2, :],
                 in_=support[n : n + 2].rearrange("n (p j) h w -> p n (j h w)", j=PACK),
             )
+            if n == 2:
+                nc.sync.dma_start(out=wv_sb[:], in_=Wv)
 
         ident = keep.tile([P, P], F32, name="ident")
         make_identity(nc, ident[:])
@@ -110,15 +116,20 @@ def tile_crossattention_pa_kernel(tc, query, support, Wk, Wv, out):
         sf_packed = [packed("sf%d" % half, NS * P) for half in range(2)]
         key_packed = [packed("key%d" % half, NS * P) for half in range(2)]
 
-        def quantise_support(half, group):
+        sf_grouped = {}
+
+        def group_support(half, group):
             n0 = group * GROUP
             grouped = stage.tile([P, GROUP * P * PACK], BF16, name="sf_grouped", tag="sf_grouped", align_bytes=64)
+            sf_grouped[half, group] = grouped
             rows = sf_sb[:, n0 : n0 + GROUP, :].rearrange("p n (t h c i) -> p h n c t i", t=PACK, h=2, i=4)
             nc.vector.tensor_copy(
                 out=grouped[:].rearrange("p (n c i t) -> p n c t i", n=GROUP, i=4, t=PACK), in_=rows[:, half]
             )
-            cols = slice(n0 * P, (n0 + GROUP) * P)
-            quantise(sf_packed[half][0][:, cols], sf_packed[half][1][:, cols], grouped[:])
+
+        def quantise_support(half, group):
+            cols = slice(group * GROUP * P, (group + 1) * GROUP * P)
+            quantise(sf_packed[half][0][:, cols], sf_packed[half][1][:, cols], sf_grouped[half, group][:])
 
         def project_keys(half, group, tag):
             grouped = stage.tile([P, GROUP * P * PACK], BF16, name="key_grouped", tag="key_grouped", align_bytes=64)
@@ -133,10 +144,11 @@ def tile_crossattention_pa_kernel(tc, query, support, Wk, Wv, out):
             quantise(key_packed[half][0][:, cols], key_packed[half][1][:, cols], grouped[:])
 
         qf_grouped = keep.tile([P, NB * 256 * PACK], BF16, name="qf_grouped", align_bytes=64)
-        nc.vector.tensor_copy(
-            out=qf_grouped[:].rearrange("p (b c i t) -> p b c t i", b=NB, i=4, t=PACK),
-            in_=q_sb[:].rearrange("p b (t c i) -> p b c t i", t=PACK, i=4),
-        )
+        for b in range(NB):
+            nc.vector.tensor_copy(
+                out=qf_grouped[:, b * 1024 : (b + 1) * 1024].rearrange("p (c i t) -> p c t i", i=4, t=PACK),
+                in_=q_sb[:, b, :].rearrange("p (t c i) -> p c t i", t=PACK, i=4),
+            )
         quantise(wk_codes[:], wk_scales[:], wk_grouped[:])
         qf_codes, qf_scales = packed("qf", NB * 256)
         quantise(qf_codes[:], qf_scales[:], qf_grouped[:])
@@ -145,6 +157,11 @@ def tile_crossattention_pa_kernel(tc, query, support, Wk, Wv, out):
         for piece in range(2 * NB):
             round_and_group(q_by_piece[:, piece], project(qf_codes, qf_scales, piece, "scores"))
         q_codes, q_scales = packed("q", NB * 256)
+
+        key_grouped = {}
+        group_support(0, 0)
+        quantise_support(0, 0)
+        key_grouped[0] = project_keys(0, 0, "scores")
 
         wv_words = wv_sb[:].bitcast(F32).rearrange("p (w u) -> p w u", u=2)
         wv_turned = psum.tile([P, 2, P], F32, name="wv_turned", tag="short")
@@ -157,17 +174,24 @@ def tile_crossattention_pa_kernel(tc, query, support, Wk, Wv, out):
         )
         wv_codes, wv_scales = packed("wv", P)
 
-        key_grouped = {}
-        for turn in range(GROUPS + 2):
-            if turn < GROUPS:
-                quantise_support(0, turn)
-                key_grouped[turn] = project_keys(0, turn, "scores")
-            if turn == 1:
-                quantise(q_codes[:], q_scales[:], q_grouped[:])
-            if turn >= GROUPS:
-                quantise_support(1, turn - GROUPS)
-            if turn >= 2:
-                quantise_keys(0, turn - 2, key_grouped[turn - 2])
+        group_support(0, 1)
+        quantise(q_codes[:], q_scales[:], q_grouped[:])
+        quantise_support(0, 1)
+        key_grouped[1] = project_keys(0, 1, "scores")
+        group_support(0, 2)
+        quantise_keys(0, 0, key_grouped[0])
+        quantise_support(0, 2)
+        key_grouped[2] = project_keys(0, 2, "scores")
+        group_support(0, 3)
+        group_support(1, 0)
+        quantise_support(0, 3)
+        key_grouped[3] = project_keys(0, 3, "scores")
+        quantise_support(1, 0)
+        quantise_keys(0, 1, key_grouped[1])
+        group_support(1, 1)
+        quantise_keys(0, 2, key_grouped[2])
+        quantise_support(1, 1)
+        quantise_keys(0, 3, key_grouped[3])
         quantise(wv_codes[:], wv_scales[:], wv_grouped[:])
 
         val_t = [keep.tile([P, NS, P], F32, name="val_t%d" % half) for half in range(2)]
@@ -257,25 +281,34 @@ def tile_crossattention_pa_kernel(tc, query, support, Wk, Wv, out):
             four_images = exps[unit][:, j * GROUP : (j + 1) * GROUP, :]
             nc.scalar.activation(out=four_images, in_=four_images, func=ACT.Exp, scale=inv_sqrt)
 
-        def sum_over_images(unit):
-            z_turned[unit] = psum.tile([P, P], F32, name="z_turned", tag="zsum", bufs=1)
-            order = [j * GROUP + g for j in (1, 2, 3, 0) for g in range(GROUP)]
-            for n in order:
-                nc.tensor.matmul(
-                    out=z_turned[unit][:],
-                    lhsT=exps[unit][:, n, :],
-                    rhs=ident[:],
-                    is_transpose=True,
-                    start=(n == order[0]),
-                    stop=(n == order[-1]),
-                )
+        EXP_ORDER = (1, 2, 3, 0)
+
+        def sum_over_images(unit, groups=EXP_ORDER):
+            if groups[0] == EXP_ORDER[0]:
+                if unit == UNITS - 1:
+                    z_turned[unit] = psum.tile([P, P], F32, name="z_last", tag="scores", bufs=3)
+                else:
+                    z_turned[unit] = psum.tile([P, P], F32, name="z_turned", tag="zsum", bufs=1)
+            for j in groups:
+                for n in range(j * GROUP, (j + 1) * GROUP):
+                    nc.tensor.matmul(
+                        out=z_turned[unit][:],
+                        lhsT=exps[unit][:, n, :],
+                        rhs=ident[:],
+                        is_transpose=True,
+                        start=(n == EXP_ORDER[0] * GROUP),
+                        stop=(n == EXP_ORDER[-1] * GROUP + GROUP - 1),
+                    )
 
         def reciprocal(unit):
             r_turned[unit] = work.tile([P, P], F32, name="r_turned", tag="r_turned")
             nc.vector.reciprocal(out=r_turned[unit][:], in_=z_turned[unit][:])
 
         def reciprocal_back(unit):
-            r_psum[unit] = psum.tile([P, P], F32, name="r_psum", tag="recip", bufs=1)
+            if unit == UNITS - 1:
+                r_psum[unit] = psum.tile([P, P], F32, name="r_last_psum", tag="scores", bufs=3)
+            else:
+                r_psum[unit] = psum.tile([P, P], F32, name="r_psum", tag="recip", bufs=1)
             nc.tensor.transpose(r_psum[unit][:], r_turned[unit][:], ident[:])
 
         def reciprocal_out(unit):
@@ -359,9 +392,10 @@ def tile_crossattention_pa_kernel(tc, query, support, Wk, Wv, out):
                     op0=ALU.mult,
                 )
 
-        def add_products(pair):
-            results[pair] = psum.tile([P, P], F32, name="result", tag="short")
-            for n in range(NS):
+        def add_products(pair, images=range(NS)):
+            if images[0] == 0:
+                results[pair] = psum.tile([P, P], F32, name="result", tag="short")
+            for n in images:
                 nc.tensor.matmul(
                     out=results[pair][:],
                     lhsT=products[pair][:, n, :],
@@ -379,100 +413,105 @@ def tile_crossattention_pa_kernel(tc, query, support, Wk, Wv, out):
 
         scores(0, (0,))
         copy_bank0(0)
-        scores(0, (1, 2, 3))
+        scores(0, (1, 2))
         late_keys = {0: project_keys(1, 0, "short")}
+        scores(0, (3,))
+        scores(1, (0,))
+        copy_bank0(1)
         LAST = UNITS - 1
-        for slot in range(UNITS + 1):
+        LATE_PRODUCTS = 6
+        for slot in range(UNITS):
             unit, last, older = slot, slot - 1, slot - 2
-            live, live_last, live_older = unit < UNITS, 0 <= last < UNITS, 0 <= older < LAST - 1
+            live_last, live_older = last >= 0, older >= 0
             pair = pair_due(slot, 4)
             if live_last:
                 sum_over_images(last)
-            if unit + 1 < UNITS:
-                scores(unit + 1, (0,))
-                copy_bank0(unit + 1)
             if pair is not None:
                 pair_sum_turn(pair)
+            if slot == LAST:
+                add_products(0)
+                store(0)
             if slot < 3:
                 late_keys[slot + 1] = project_keys(1, slot + 1, "short")
-            if live:
-                maximum_of_bank(unit, 1)
+            maximum_of_bank(unit, 1)
+            if slot < 2:
+                group_support(1, slot + 2)
             if live_older:
                 multiply(nc.gpsimd, older, 9, 7)
                 multiply(nc.vector, older, 0, 1)
-            if live:
-                maximum_of_bank(unit, 2)
+            maximum_of_bank(unit, 2)
+            if slot < 2:
+                quantise_support(1, slot + 2)
             if live_older:
                 multiply(nc.vector, older, 1, 1)
                 add_strips(older, 0, 9)
-            if live:
-                maximum_of_bank(unit, 3)
-                maximum_of_four(unit)
-                subtract(nc.gpsimd, unit, 0, bank0_copy[unit])
+            maximum_of_bank(unit, 3)
+            if slot < 3:
+                quantise_keys(1, slot, late_keys[slot])
+            maximum_of_four(unit)
+            subtract(nc.gpsimd, unit, 0, bank0_copy[unit])
             if live_last and slot < LAST:
                 reciprocal(last)
                 reciprocal_back(last)
                 reciprocal_out(last)
             if pair is not None:
                 weights_out(pair)
-            if live:
-                for j in (1, 2, 3):
-                    subtract(nc.vector, unit, j, banks[unit][j])
-            if live_last and slot >= LAST:
-                reciprocal(last)
+            for j in (1, 2, 3):
+                subtract(nc.vector, unit, j, banks[unit][j])
+            if slot == 2:
+                quantise_keys(1, 3, late_keys[3])
             if live_older:
                 add_strips(older, 9, 7)
             if unit + 1 < UNITS:
                 scores(unit + 1, (1, 2, 3))
-            if live_last and slot >= LAST:
-                reciprocal_back(last)
-            if live:
-                for j in (1, 2, 3, 0):
-                    exponentials(unit, j)
-            if slot == LAST:
-                reciprocal_out(last)
+            if unit + 2 < UNITS:
+                scores(unit + 2, (0,))
+            for j in EXP_ORDER:
+                exponentials(unit, j)
+            if unit + 2 < UNITS:
+                copy_bank0(unit + 2)
             if live_last and slot < LAST:
                 multiply(nc.gpsimd, last, 2, 7)
-            if slot == LAST:
-                multiply(nc.vector, last, 0, 4)
-                multiply(nc.vector, last, 4, 4)
-                multiply(nc.gpsimd, last, 8, 4)
-                multiply(nc.gpsimd, last, 12, 4)
-            if pair_due(slot, 3) is not None:
+            if pair_due(slot, 3) is not None and slot < LAST:
                 pair_sum_copy(pair_due(slot, 3))
-            if slot in (2, 3):
-                values(0, 2 * slot - 4)
-                values(0, 2 * slot - 3)
-            if slot in (4, 5, 6):
-                values(1, slot - 4)
+            values(slot // 4, slot % 4)
+            if slot == 4:
+                weigh_on_scalar(0, range(0, NS // 2))
+            if slot == 5:
+                weigh_on_scalar(0, range(NS // 2, NS))
             if slot == 6:
-                values(1, 3)
-            if slot in (4, 6):
-                weigh_on_scalar((slot - 4) // 2, range(0, NS // 2))
-            if slot in (5, 7):
-                weigh_on_scalar((slot - 5) // 2, range(NS // 2, NS))
-            if slot == LAST + 1:
-                for first in range(0, STRIPS, 4):
-                    multiply(nc.vector, LAST, first, 4)
-                weigh_on_gpsimd(2, 8)
-                weigh_on_scalar(2, range(8, NS))
-                add_strips(LAST - 1, 0, STRIPS)
-                add_strips(LAST, 0, STRIPS)
-            if slot < 2:
-                quantise_support(1, slot + 2)
-            if slot < 3:
-                quantise_keys(1, slot, late_keys[slot])
-            if slot == 2:
-                quantise_keys(1, 3, late_keys[3])
-            if slot in (6, 8):
-                add_products((slot - 6) // 2)
-                store((slot - 6) // 2)
+                weigh_on_scalar(1, range(0, LATE_PRODUCTS))
+        sum_over_images(LAST, EXP_ORDER[:3])
+        reciprocal(LAST - 1)
+        reciprocal_back(LAST - 1)
+        sum_over_images(LAST, EXP_ORDER[3:])
+        reciprocal_out(LAST - 1)
+        pair_sum_copy(2)
+        multiply(nc.gpsimd, LAST - 1, 8, 4)
+        multiply(nc.gpsimd, LAST - 1, 12, 4)
+        weigh_on_vector(1, range(LATE_PRODUCTS, NS))
+        pair_sum_turn(2)
+        weights_out(2)
+        reciprocal(LAST)
+        reciprocal_back(LAST)
+        add_products(1, range(0, 8))
+        reciprocal_out(LAST)
+        multiply(nc.gpsimd, LAST, 12, 4)
+        multiply(nc.vector, LAST - 1, 0, 4)
+        multiply(nc.vector, LAST - 1, 4, 4)
+        for first in range(0, 12, 4):
+            multiply(nc.vector, LAST, first, 4)
+        weigh_on_scalar(2, range(NS))
+        add_strips(LAST - 1, 0, STRIPS)
+        add_strips(LAST, 0, STRIPS)
+        add_products(1, range(8, NS))
         pair_sum_copy(3)
+        store(1)
         pair_sum_turn(3)
         weights_out(3)
+        add_products(2)
         weigh_on_vector(3, range(0, 11))
         weigh_on_scalar(3, range(11, NS))
-        add_products(2)
         add_products(3)
         store(2)
         store(3)

@@ -437,14 +437,14 @@ def tile_crossattention_pa_kernel(tc, query, support, Wk, Wv, out):
             if slot < 2:
                 group_support(1, slot + 2)
             if live_older:
-                multiply(nc.gpsimd, older, 9, 7)
-                multiply(nc.vector, older, 0, 1)
+                multiply(nc.gpsimd, older, 10, 6)
+                multiply(nc.vector, older, 0, 2)
             maximum_of_bank(unit, 2)
             if slot < 2:
                 quantise_support(1, slot + 2)
             if live_older:
-                multiply(nc.vector, older, 1, 1)
-                add_strips(older, 0, 9)
+                multiply(nc.vector, older, 2, 2)
+                add_strips(older, 0, 10)
             maximum_of_bank(unit, 3)
             if slot < 3:
                 quantise_keys(1, slot, late_keys[slot])
@@ -461,7 +461,7 @@ def tile_crossattention_pa_kernel(tc, query, support, Wk, Wv, out):
             if slot == 2:
                 quantise_keys(1, 3, late_keys[3])
             if live_older:
-                add_strips(older, 9, 7)
+                add_strips(older, 10, 6)
             if unit + 1 < UNITS:
                 scores(unit + 1, (1, 2, 3))
             if unit + 2 < UNITS:
@@ -471,7 +471,7 @@ def tile_crossattention_pa_kernel(tc, query, support, Wk, Wv, out):
             if unit + 2 < UNITS:
                 copy_bank0(unit + 2)
             if live_last and slot < LAST:
-                multiply(nc.gpsimd, last, 2, 7)
+                multiply(nc.gpsimd, last, 4, 6)
             if pair_due(slot, 3) is not None and slot < LAST:
                 pair_sum_copy(pair_due(slot, 3))
             values(slot // 4, slot % 4)

@@ -437,14 +437,14 @@ def tile_crossattention_pa_kernel(tc, query, support, Wk, Wv, out):
             if slot < 2:
                 group_support(1, slot + 2)
             if live_older:
-                multiply(nc.gpsimd, older, 10, 6)
-                multiply(nc.vector, older, 0, 2)
+                multiply(nc.gpsimd, older, 11, 5)
+                multiply(nc.vector, older, 0, 3)
             maximum_of_bank(unit, 2)
             if slot < 2:
                 quantise_support(1, slot + 2)
             if live_older:
-                multiply(nc.vector, older, 2, 2)
-                add_strips(older, 0, 10)
+                multiply(nc.vector, older, 3, 3)
+                add_strips(older, 0, 11)
             maximum_of_bank(unit, 3)
             if slot < 3:
                 quantise_keys(1, slot, late_keys[slot])
@@ -461,7 +461,7 @@ def tile_crossattention_pa_kernel(tc, query, support, Wk, Wv, out):
             if slot == 2:
                 quantise_keys(1, 3, late_keys[3])
             if live_older:
-                add_strips(older, 10, 6)
+                add_strips(older, 11, 5)
             if unit + 1 < UNITS:
                 scores(unit + 1, (1, 2, 3))
             if unit + 2 < UNITS:
@@ -471,7 +471,7 @@ def tile_crossattention_pa_kernel(tc, query, support, Wk, Wv, out):
             if unit + 2 < UNITS:
                 copy_bank0(unit + 2)
             if live_last and slot < LAST:
-                multiply(nc.gpsimd, last, 4, 6)
+                multiply(nc.gpsimd, last, 6, 5)
             if pair_due(slot, 3) is not None and slot < LAST:
                 pair_sum_copy(pair_due(slot, 3))
             values(slot // 4, slot % 4)

@@ -345,6 +345,11 @@ def tile_crossattention_pa_kernel(tc, query, support, Wk, Wv, out):
                 )
                 added[pair] += 1
 
+        def keep_warm(count):
+            scrap = psum.tile([P, 512], F32, name="scrap", tag="scores", bufs=3)
+            for i in range(count):
+                nc.tensor.matmul(out=scrap[:], lhsT=wk_sb[:, 0:P], rhs=wk_sb[:, 0:512], start=True, stop=True)
+
         summed = {}
         turned_sum = {}
 
@@ -481,6 +486,7 @@ def tile_crossattention_pa_kernel(tc, query, support, Wk, Wv, out):
                 weigh_on_scalar(0, range(NS // 2, NS))
             if slot == 6:
                 weigh_on_scalar(1, range(0, LATE_PRODUCTS))
+        keep_warm(2)
         sum_over_images(LAST, EXP_ORDER[:3])
         reciprocal(LAST - 1)
         reciprocal_back(LAST - 1)
@@ -490,6 +496,7 @@ def tile_crossattention_pa_kernel(tc, query, support, Wk, Wv, out):
         multiply(nc.gpsimd, LAST - 1, 8, 4)
         multiply(nc.gpsimd, LAST - 1, 12, 4)
         weigh_on_vector(1, range(LATE_PRODUCTS, NS))
+        keep_warm(2)
         pair_sum_turn(2)
         weights_out(2)
         reciprocal(LAST)
@@ -502,16 +509,20 @@ def tile_crossattention_pa_kernel(tc, query, support, Wk, Wv, out):
         for first in range(0, 12, 4):
             multiply(nc.vector, LAST, first, 4)
         weigh_on_scalar(2, range(NS))
+        keep_warm(2)
         add_strips(LAST - 1, 0, STRIPS)
+        keep_warm(2)
         add_strips(LAST, 0, STRIPS)
         add_products(1, range(8, NS))
         pair_sum_copy(3)
         store(1)
+        keep_warm(2)
         pair_sum_turn(3)
         weights_out(3)
         add_products(2)
         weigh_on_vector(3, range(0, 11))
         weigh_on_scalar(3, range(11, NS))
+        keep_warm(2)
         add_products(3)
         store(2)
         store(3)

@@ -61,6 +61,9 @@ def tile_crossattention_pa_kernel(tc, query, support, Wk, Wv, out):
 
         ident = keep.tile([P, P], F32, name="ident")
         make_identity(nc, ident[:])
+        first_scrap = psum.tile([P, P], F32, name="first_scrap", tag="scores", bufs=3)
+        for i in range(3):
+            nc.tensor.matmul(out=first_scrap[:], lhsT=ident[:], rhs=ident[:], start=True, stop=True)
         warm = keep.tile([P, 1], F32, name="warm")
         nc.vector.memset(warm[:], 0.0)
         nc.scalar.activation(out=warm[:], in_=warm[:], func=ACT.Exp)
@@ -345,8 +348,8 @@ def tile_crossattention_pa_kernel(tc, query, support, Wk, Wv, out):
                 )
                 added[pair] += 1
 
-        def keep_warm(count):
-            scrap = psum.tile([P, 512], F32, name="scrap", tag="scores", bufs=3)
+        def keep_warm(count, tag="scores"):
+            scrap = psum.tile([P, 512], F32, name="scrap", tag=tag, bufs=(3 if tag == "scores" else 2))
             for i in range(count):
                 nc.tensor.matmul(out=scrap[:], lhsT=wk_sb[:, 0:P], rhs=wk_sb[:, 0:512], start=True, stop=True)
 
@@ -397,7 +400,15 @@ def tile_crossattention_pa_kernel(tc, query, support, Wk, Wv, out):
                     op0=ALU.mult,
                 )
 
-        def add_products(pair, images=range(NS)):
+        def fold_products(engine, pair, first, count):
+            engine.tensor_tensor(
+                out=products[pair][:, first : first + count, :],
+                in0=products[pair][:, first : first + count, :],
+                in1=products[pair][:, first + NS // 2 : first + NS // 2 + count, :],
+                op=ALU.add,
+            )
+
+        def add_products(pair, images=range(NS), total=NS):
             if images[0] == 0:
                 results[pair] = psum.tile([P, P], F32, name="result", tag="short")
             for n in images:
@@ -407,7 +418,7 @@ def tile_crossattention_pa_kernel(tc, query, support, Wk, Wv, out):
                     rhs=ident[:],
                     is_transpose=True,
                     start=(n == 0),
-                    stop=(n == NS - 1),
+                    stop=(n == total - 1),
                 )
 
         def store(pair):
@@ -424,32 +435,31 @@ def tile_crossattention_pa_kernel(tc, query, support, Wk, Wv, out):
         scores(1, (0,))
         copy_bank0(1)
         LAST = UNITS - 1
-        LATE_PRODUCTS = 6
+        LATE_PRODUCTS = 12
         for slot in range(UNITS):
             unit, last, older = slot, slot - 1, slot - 2
             live_last, live_older = last >= 0, older >= 0
             pair = pair_due(slot, 4)
             if live_last:
                 sum_over_images(last)
+            if live_last:
+                keep_warm(2, "short")
             if pair is not None:
                 pair_sum_turn(pair)
-            if slot == LAST:
-                add_products(0)
-                store(0)
             if slot < 3:
                 late_keys[slot + 1] = project_keys(1, slot + 1, "short")
             maximum_of_bank(unit, 1)
             if slot < 2:
                 group_support(1, slot + 2)
             if live_older:
-                multiply(nc.gpsimd, older, 11, 5)
-                multiply(nc.vector, older, 0, 3)
+                multiply(nc.gpsimd, older, 10, 6)
+                multiply(nc.vector, older, 0, 2)
             maximum_of_bank(unit, 2)
             if slot < 2:
                 quantise_support(1, slot + 2)
             if live_older:
-                multiply(nc.vector, older, 3, 3)
-                add_strips(older, 0, 11)
+                multiply(nc.vector, older, 2, 2)
+                add_strips(older, 0, 10)
             maximum_of_bank(unit, 3)
             if slot < 3:
                 quantise_keys(1, slot, late_keys[slot])
@@ -466,7 +476,7 @@ def tile_crossattention_pa_kernel(tc, query, support, Wk, Wv, out):
             if slot == 2:
                 quantise_keys(1, 3, late_keys[3])
             if live_older:
-                add_strips(older, 11, 5)
+                add_strips(older, 10, 6)
             if unit + 1 < UNITS:
                 scores(unit + 1, (1, 2, 3))
             if unit + 2 < UNITS:
@@ -476,7 +486,7 @@ def tile_crossattention_pa_kernel(tc, query, support, Wk, Wv, out):
             if unit + 2 < UNITS:
                 copy_bank0(unit + 2)
             if live_last and slot < LAST:
-                multiply(nc.gpsimd, last, 6, 5)
+                multiply(nc.gpsimd, last, 4, 6)
             if pair_due(slot, 3) is not None and slot < LAST:
                 pair_sum_copy(pair_due(slot, 3))
             values(slot // 4, slot % 4)
@@ -486,6 +496,7 @@ def tile_crossattention_pa_kernel(tc, query, support, Wk, Wv, out):
                 weigh_on_scalar(0, range(NS // 2, NS))
             if slot == 6:
                 weigh_on_scalar(1, range(0, LATE_PRODUCTS))
+        fold_products(nc.gpsimd, 0, 0, 8)
         keep_warm(2)
         sum_over_images(LAST, EXP_ORDER[:3])
         reciprocal(LAST - 1)
@@ -499,27 +510,31 @@ def tile_crossattention_pa_kernel(tc, query, support, Wk, Wv, out):
         keep_warm(2)
         pair_sum_turn(2)
         weights_out(2)
+        add_products(0, range(8), 8)
         reciprocal(LAST)
         reciprocal_back(LAST)
-        add_products(1, range(0, 8))
+        add_products(1, range(0, 10))
         reciprocal_out(LAST)
+        store(0)
         multiply(nc.gpsimd, LAST, 12, 4)
         multiply(nc.vector, LAST - 1, 0, 4)
         multiply(nc.vector, LAST - 1, 4, 4)
         for first in range(0, 12, 4):
             multiply(nc.vector, LAST, first, 4)
-        weigh_on_scalar(2, range(NS))
+        weigh_on_scalar(2, (0, 8, 1, 9, 2, 10, 3, 11, 4, 12, 5, 13, 6, 14, 7, 15))
+        fold_products(nc.vector, 2, 0, 4)
+        fold_products(nc.vector, 2, 4, 4)
         keep_warm(2)
         add_strips(LAST - 1, 0, STRIPS)
         keep_warm(2)
         add_strips(LAST, 0, STRIPS)
-        add_products(1, range(8, NS))
+        add_products(1, range(10, NS))
         pair_sum_copy(3)
         store(1)
         keep_warm(2)
         pair_sum_turn(3)
         weights_out(3)
-        add_products(2)
+        add_products(2, range(8), 8)
         weigh_on_vector(3, range(0, 11))
         weigh_on_scalar(3, range(11, NS))
         keep_warm(2)

import math
from contextlib import ExitStack

import concourse.mybir as mybir
from concourse.masks import make_identity

F32 = mybir.dt.float32
BF16 = mybir.dt.bfloat16
U32 = mybir.dt.uint32
U8 = mybir.dt.uint8
FP8X4 = mybir.dt.float8_e4m3fn_x4
ALU = mybir.AluOpType
ACT = mybir.ActivationFunctionType
AX = mybir.AxisListType

P = 128
PACK = 4
NB = 2
NS = 16
GROUP = 4
GROUPS = NS // GROUP
UNITS = 8
PAIRS = UNITS // 2
TAIL = 8
STRIPS = P // TAIL
FLOPS = 2 * 512 * 512 * 256 * (NB + NS) + 2 * 128 * 512 * 256 * NS + 2 * 512 * 256 * 256 * NB * NS


def pair_due(slot, lag):
    pair, rest = divmod(slot - lag, 2)
    return pair if rest == 0 and 0 <= pair < PAIRS else None


def tile_crossattention_pa_kernel(tc, query, support, Wk, Wv, out):
    nc = tc.nc
    with ExitStack() as ctx:
        keep = ctx.enter_context(tc.tile_pool(name="keep", bufs=1))
        stage = ctx.enter_context(tc.tile_pool(name="stage", bufs=3))
        work = ctx.enter_context(tc.tile_pool(name="work", bufs=2))
        psum = ctx.enter_context(tc.psum_pool(name="psum", bufs=2))
        ctx.enter_context(tc.manual_schedule())

        wk_sb = keep.tile([P, PACK * 512], BF16, name="wk_sb")
        for h in range(2):
            nc.sync.dma_start(
                out=wk_sb[:, h * 1024 : (h + 1) * 1024],
                in_=Wk.rearrange("(p h m) d -> p h (m d)", h=2, m=2)[:, h, :],
            )
        q_sb = keep.tile([P, NB, PACK * 256], BF16, name="q_sb")
        for b in range(NB):
            nc.sync.dma_start(out=q_sb[:, b, :], in_=query[b].rearrange("(p j) h w -> p (j h w)", j=PACK))
        wv_sb = keep.tile([P, 512], BF16, name="wv_sb")
        sf_sb = keep.tile([P, NS, PACK * 256], BF16, name="sf_sb")
        for n in range(0, NS, 2):
            nc.sync.dma_start(
                out=sf_sb[:, n : n + 2, :],
                in_=support[n : n + 2].rearrange("n (p j) h w -> p n (j h w)", j=PACK),
            )
            if n == 2:
                nc.sync.dma_start(out=wv_sb[:], in_=Wv)

        ident = keep.tile([P, P], F32, name="ident")
        make_identity(nc, ident[:])
        first_scrap = psum.tile([P, P], F32, name="first_scrap", tag="scores", bufs=3)
        for i in range(3):
            nc.tensor.matmul(out=first_scrap[:], lhsT=ident[:], rhs=ident[:], start=True, stop=True)
        warm = keep.tile([P, 1], F32, name="warm")
        nc.vector.memset(warm[:], 0.0)
        nc.scalar.activation(out=warm[:], in_=warm[:], func=ACT.Exp)
        same_image = keep.tile([P, NS], F32, name="same_image")
        nc.vector.tensor_reduce(
            out=same_image[:], in_=ident[:].rearrange("p (n j) -> p n j", j=TAIL), axis=AX.X, op=ALU.add
        )

        def quantise(codes, scales, grouped):
            nc.vector.quantize_mx(out=codes.bitcast(FP8X4), scales=scales, in_=grouped)

        def packed(name, columns):
            codes = keep.tile([P, columns], U32, name=name + "_codes", align_bytes=64)
            scales = keep.tile([P, columns], U8, name=name + "_scales", align_bytes=64)
            return codes, scales

        wk_words = wk_sb[:].bitcast(F32).rearrange("p (m w u) -> p m w u", m=PACK, u=2)
        wk_grouped = keep.tile([P, PACK * 512], BF16, name="wk_grouped", align_bytes=64)
        wk_grouped_words = wk_grouped[:].bitcast(F32).rearrange("p (m c u) -> p m c u", m=PACK, u=2)
        wk_turned = []
        for first in (0, 2):
            bank = psum.tile([P, 2, 2, P], F32, name="wk_turned", tag="short")
            for m in range(2):
                for u in range(2):
                    nc.tensor.transpose(bank[:, m, u, :], wk_words[:, first + m, :, u], ident[:])
            wk_turned.append(bank)
        for first in (0, 2):
            nc.scalar.copy(
                out=wk_grouped_words[:, first : first + 2, :, :],
                in_=wk_turned[first // 2][:].rearrange("p m u c -> p m c u"),
            )
        wk_codes, wk_scales = packed("wk", 512)

        def project(codes, scales, piece, tag):
            bank = psum.tile([P, PACK, P], F32, name="projected", tag=tag, bufs=(3 if tag == "scores" else 2))
            cols = slice(piece * P, (piece + 1) * P)
            for m in range(PACK):
                chunk = slice(m * P, (m + 1) * P)
                nc.tensor.matmul_mx(
                    out=bank[:, m, :],
                    lhsT=wk_codes[:, chunk].bitcast(FP8X4),
                    lhsT_scale=wk_scales[:, chunk],
                    rhs=codes[:, cols].bitcast(FP8X4),
                    rhs_scale=scales[:, cols],
                    start=True,
                    stop=True,
                )
            return bank

        def round_and_group(grouped, bank):
            nc.scalar.copy(out=grouped, in_=bank[:].rearrange("p m w -> p w m"))

        sf_packed = [packed("sf%d" % half, NS * P) for half in range(2)]
        key_packed = [packed("key%d" % half, NS * P) for half in range(2)]

        sf_grouped = {}

        def group_support(half, group):
            n0 = group * GROUP
            grouped = stage.tile([P, GROUP * P * PACK], BF16, name="sf_grouped", tag="sf_grouped", align_bytes=64)
            sf_grouped[half, group] = grouped
            rows = sf_sb[:, n0 : n0 + GROUP, :].rearrange("p n (t h c i) -> p h n c t i", t=PACK, h=2, i=4)
            nc.vector.tensor_copy(
                out=grouped[:].rearrange("p (n c i t) -> p n c t i", n=GROUP, i=4, t=PACK), in_=rows[:, half]
            )

        def quantise_support(half, group):
            cols = slice(group * GROUP * P, (group + 1) * GROUP * P)
            quantise(sf_packed[half][0][:, cols], sf_packed[half][1][:, cols], sf_grouped[half, group][:])

        def project_keys(half, group, tag):
            grouped = stage.tile([P, GROUP * P * PACK], BF16, name="key_grouped", tag="key_grouped", align_bytes=64)
            by_image = grouped[:].rearrange("p (g w m) -> p g w m", g=GROUP, m=PACK)
            for g in range(GROUP):
                bank = project(sf_packed[half][0], sf_packed[half][1], group * GROUP + g, tag)
                round_and_group(by_image[:, g], bank)
            return grouped

        def quantise_keys(half, group, grouped):
            cols = slice(group * GROUP * P, (group + 1) * GROUP * P)
            quantise(key_packed[half][0][:, cols], key_packed[half][1][:, cols], grouped[:])

        qf_grouped = keep.tile([P, NB * 256 * PACK], BF16, name="qf_grouped", align_bytes=64)
        for b in range(NB):
            nc.vector.tensor_copy(
                out=qf_grouped[:, b * 1024 : (b + 1) * 1024].rearrange("p (c i t) -> p c t i", i=4, t=PACK),
                in_=q_sb[:, b, :].rearrange("p (t c i) -> p c t i", t=PACK, i=4),
            )
        quantise(wk_codes[:], wk_scales[:], wk_grouped[:])
        qf_codes, qf_scales = packed("qf", NB * 256)
        quantise(qf_codes[:], qf_scales[:], qf_grouped[:])
        q_grouped = keep.tile([P, NB * 256 * PACK], BF16, name="q_grouped", align_bytes=64)
        q_by_piece = q_grouped[:].rearrange("p (g w m) -> p g w m", g=2 * NB, m=PACK)
        for piece in range(2 * NB):
            round_and_group(q_by_piece[:, piece], project(qf_codes, qf_scales, piece, "scores"))
        q_codes, q_scales = packed("q", NB * 256)

        key_grouped = {}
        group_support(0, 0)
        quantise_support(0, 0)
        key_grouped[0] = project_keys(0, 0, "scores")

        wv_words = wv_sb[:].bitcast(F32).rearrange("p (w u) -> p w u", u=2)
        wv_turned = psum.tile([P, 2, P], F32, name="wv_turned", tag="short")
        for u in range(2):
            nc.tensor.transpose(wv_turned[:, u, :], wv_words[:, :, u], ident[:])
        wv_grouped = keep.tile([P, P * PACK], BF16, name="wv_grouped", align_bytes=64)
        nc.scalar.copy(
            out=wv_grouped[:].bitcast(F32).rearrange("p (c u) -> p c u", u=2),
            in_=wv_turned[:].rearrange("p u c -> p c u"),
        )
        wv_codes, wv_scales = packed("wv", P)

        group_support(0, 1)
        quantise(q_codes[:], q_scales[:], q_grouped[:])
        quantise_support(0, 1)
        key_grouped[1] = project_keys(0, 1, "scores")
        group_support(0, 2)
        quantise_keys(0, 0, key_grouped[0])
        quantise_support(0, 2)
        key_grouped[2] = project_keys(0, 2, "scores")
        group_support(0, 3)
        group_support(1, 0)
        quantise_support(0, 3)
        key_grouped[3] = project_keys(0, 3, "scores")
        quantise_support(1, 0)
        quantise_keys(0, 1, key_grouped[1])
        group_support(1, 1)
        quantise_keys(0, 2, key_grouped[2])
        quantise_support(1, 1)
        quantise_keys(0, 3, key_grouped[3])
        quantise(wv_codes[:], wv_scales[:], wv_grouped[:])

        val_t = [keep.tile([P, NS, P], F32, name="val_t%d" % half) for half in range(2)]

        def values(half, group):
            bank = psum.tile([P, GROUP, P], F32, name="val_bank", tag="short")
            for g in range(GROUP):
                cols = slice((group * GROUP + g) * P, (group * GROUP + g + 1) * P)
                nc.tensor.matmul_mx(
                    out=bank[:, g, :],
                    lhsT=sf_packed[half][0][:, cols].bitcast(FP8X4),
                    lhsT_scale=sf_packed[half][1][:, cols],
                    rhs=wv_codes[:].bitcast(FP8X4),
                    rhs_scale=wv_scales[:],
                    start=True,
                    stop=True,
                )
            nc.scalar.copy(out=val_t[half][:, group * GROUP : (group + 1) * GROUP, :], in_=bank[:])

        inv_sqrt = 1.0 / math.sqrt(512.0)
        banks = {}
        bank0_copy = {}
        maxima = {}
        exps = {}
        z_turned = {}
        r_turned = {}
        r_psum = {}
        r_last = {}
        strips = {}
        pair_sum = {}
        weights = {}
        products = {}
        results = {}

        def scores(unit, which):
            half, piece = unit // 4, unit % 4
            q_cols = slice(piece * P, (piece + 1) * P)
            codes, scales = key_packed[half]
            if 0 in which:
                banks[unit] = []
            for j in which:
                if j == 0:
                    bank = psum.tile([P, GROUP, P], F32, name="scores0", tag="short")
                else:
                    bank = psum.tile([P, GROUP, P], F32, name="scores", tag="scores", bufs=3)
                for g in range(GROUP):
                    cols = slice((j * GROUP + g) * P, (j * GROUP + g + 1) * P)
                    nc.tensor.matmul_mx(
                        out=bank[:, g, :],
                        lhsT=codes[:, cols].bitcast(FP8X4),
                        lhsT_scale=scales[:, cols],
                        rhs=q_codes[:, q_cols].bitcast(FP8X4),
                        rhs_scale=q_scales[:, q_cols],
                        start=True,
                        stop=True,
                    )
                banks[unit].append(bank)

        def copy_bank0(unit):
            bank0_copy[unit] = work.tile([P, GROUP, P], F32, name="bank0_copy", tag="bank0_copy")
            nc.scalar.copy(out=bank0_copy[unit][:], in_=banks[unit][0][:])

        four = {}

        def maximum_of_bank(unit, j):
            if j == 1:
                exps[unit] = work.tile([P, NS, P], F32, name="exps", tag="exps", bufs=3)
                four[unit] = work.tile([P, GROUP, P], F32, name="max_of_banks", tag="max_of_banks")
            other = bank0_copy[unit] if j == 1 else four[unit]
            nc.vector.tensor_tensor(out=four[unit][:], in0=banks[unit][j][:], in1=other[:], op=ALU.max)

        def maximum_of_four(unit):
            maxima[unit] = work.tile([P, P], F32, name="maxima", tag="maxima")
            nc.vector.tensor_reduce(
                out=maxima[unit][:], in_=four[unit][:].rearrange("p n u -> p u n"), axis=AX.X, op=ALU.max
            )

        def subtract(engine, unit, j, source):
            engine.tensor_tensor(
                out=exps[unit][:, j * GROUP : (j + 1) * GROUP, :],
                in0=source[:],
                in1=maxima[unit][:].unsqueeze(1).to_broadcast([P, GROUP, P]),
                op=ALU.subtract,
            )

        def exponentials(unit, j):
            four_images = exps[unit][:, j * GROUP : (j + 1) * GROUP, :]
            nc.scalar.activation(out=four_images, in_=four_images, func=ACT.Exp, scale=inv_sqrt)

        EXP_ORDER = (1, 2, 3, 0)

        def sum_over_images(unit, groups=EXP_ORDER):
            if groups[0] == EXP_ORDER[0]:
                if unit == UNITS - 1:
                    z_turned[unit] = psum.tile([P, P], F32, name="z_last", tag="scores", bufs=3)
                else:
                    z_turned[unit] = psum.tile([P, P], F32, name="z_turned", tag="zsum", bufs=1)
            for j in groups:
                for n in range(j * GROUP, (j + 1) * GROUP):
                    nc.tensor.matmul(
                        out=z_turned[unit][:],
                        lhsT=exps[unit][:, n, :],
                        rhs=ident[:],
                        is_transpose=True,
                        start=(n == EXP_ORDER[0] * GROUP),
                        stop=(n == EXP_ORDER[-1] * GROUP + GROUP - 1),
                    )

        def reciprocal(unit):
            r_turned[unit] = work.tile([P, P], F32, name="r_turned", tag="r_turned")
            nc.vector.reciprocal(out=r_turned[unit][:], in_=z_turned[unit][:])

        def reciprocal_back(unit):
            if unit == UNITS - 1:
                r_psum[unit] = psum.tile([P, P], F32, name="r_last_psum", tag="scores", bufs=3)
            else:
                r_psum[unit] = psum.tile([P, P], F32, name="r_psum", tag="recip", bufs=1)
            nc.tensor.transpose(r_psum[unit][:], r_turned[unit][:], ident[:])

        def reciprocal_out(unit):
            r_last[unit] = work.tile([P, P], F32, name="r_last", tag="r_last")
            nc.scalar.copy(out=r_last[unit][:], in_=r_psum[unit][:])

        def multiply(engine, unit, first, count):
            if unit not in strips:
                strips[unit] = work.tile([P, STRIPS, NS, TAIL], F32, name="strips", tag="strips")
            us = slice(first * TAIL, (first + count) * TAIL)
            r = r_psum[unit][:, us] if engine is nc.vector else r_last[unit][:, us]
            engine.tensor_tensor(
                out=strips[unit][:, first : first + count, :, :],
                in0=exps[unit][:, :, us].rearrange("p n (g j) -> p g n j", j=TAIL),
                in1=r.rearrange("p (g j) -> p g j", j=TAIL).unsqueeze(2).to_broadcast([P, count, NS, TAIL]),
                op=ALU.mult,
            )

        added = {}

        def add_strips(unit, first, count):
            pair = unit // 2
            if pair not in pair_sum:
                pair_sum[pair] = psum.tile([P, P], F32, name="pair_sum", tag="pairsum", bufs=1)
                added[pair] = 0
            for g in range(first, first + count):
                nc.tensor.matmul(
                    out=pair_sum[pair][:],
                    lhsT=strips[unit][:, g, :, :].rearrange("p n j -> p (n j)"),
                    rhs=ident[:],
                    is_transpose=True,
                    start=(added[pair] == 0),
                    stop=(added[pair] == 2 * STRIPS - 1),
                )
                added[pair] += 1

        def keep_warm(count, tag="scores"):
            scrap = psum.tile([P, 512], F32, name="scrap", tag=tag, bufs=(3 if tag == "scores" else 2))
            for i in range(count):
                nc.tensor.matmul(out=scrap[:], lhsT=wk_sb[:, 0:P], rhs=wk_sb[:, 0:512], start=True, stop=True)

        summed = {}
        turned_sum = {}

        def pair_sum_copy(pair):
            summed[pair] = work.tile([P, P], F32, name="pair_sum_sb", tag="pair_sum_sb")
            nc.scalar.copy(out=summed[pair][:], in_=pair_sum[pair][:])

        def pair_sum_turn(pair):
            turned_sum[pair] = psum.tile([P, NS], F32, name="weights_psum", tag="short")
            nc.tensor.matmul(out=turned_sum[pair][:], lhsT=summed[pair][:], rhs=same_image[:], start=True, stop=True)

        def weights_out(pair):
            weights[pair] = work.tile([P, NS], F32, name="weights", tag="weights")
            nc.scalar.copy(out=weights[pair][:], in_=turned_sum[pair][:])

        def weigh_on_scalar(pair, images):
            if pair not in products:
                products[pair] = work.tile([P, NS, P], F32, name="products", tag="products")
            for n in images:
                nc.scalar.activation(
                    out=products[pair][:, n, :],
                    in_=val_t[pair // 2][:, n, :],
                    func=ACT.Copy,
                    scale=weights[pair][:, n : n + 1],
                )

        def weigh_on_gpsimd(pair, count):
            products[pair] = work.tile([P, NS, P], F32, name="products", tag="products")
            nc.gpsimd.tensor_tensor(
                out=products[pair][:, 0:count, :],
                in0=val_t[pair // 2][:, 0:count, :],
                in1=weights[pair][:, 0:count].unsqueeze(2).to_broadcast([P, count, P]),
                op=ALU.mult,
            )

        def weigh_on_vector(pair, images):
            if pair not in products:
                products[pair] = work.tile([P, NS, P], F32, name="products", tag="products")
            for n in images:
                nc.vector.tensor_scalar(
                    out=products[pair][:, n, :],
                    in0=val_t[pair // 2][:, n, :],
                    scalar1=weights[pair][:, n : n + 1],
                    scalar2=None,
                    op0=ALU.mult,
                )

        def fold_products(engine, pair, first, count):
            engine.tensor_tensor(
                out=products[pair][:, first : first + count, :],
                in0=products[pair][:, first : first + count, :],
                in1=products[pair][:, first + NS // 2 : first + NS // 2 + count, :],
                op=ALU.add,
            )

        def add_products(pair, images=range(NS), total=NS):
            if images[0] == 0:
                results[pair] = psum.tile([P, P], F32, name="result", tag="short")
            for n in images:
                nc.tensor.matmul(
                    out=results[pair][:],
                    lhsT=products[pair][:, n, :],
                    rhs=ident[:],
                    is_transpose=True,
                    start=(n == 0),
                    stop=(n == total - 1),
                )

        def store(pair):
            half, b = pair // 2, pair % 2
            result_sb = work.tile([P, P], F32, name="result_sb", tag="result_sb")
            nc.scalar.copy(out=result_sb[:], in_=results[pair][:])
            nc.sync.dma_start(out=out[b, :, half * P : (half + 1) * P], in_=result_sb[:])

        scores(0, (0,))
        copy_bank0(0)
        scores(0, (1, 2))
        late_keys = {0: project_keys(1, 0, "short")}
        scores(0, (3,))
        scores(1, (0,))
        copy_bank0(1)
        LAST = UNITS - 1
        LATE_PRODUCTS = 12
        for slot in range(UNITS):
            unit, last, older = slot, slot - 1, slot - 2
            live_last, live_older = last >= 0, older >= 0
            pair = pair_due(slot, 4)
            if live_last:
                sum_over_images(last)
            if live_last:
                keep_warm(2, "short")
            if pair is not None:
                pair_sum_turn(pair)
            if slot < 3:
                late_keys[slot + 1] = project_keys(1, slot + 1, "short")
            maximum_of_bank(unit, 1)
            if slot < 2:
                group_support(1, slot + 2)
            if live_older:
                multiply(nc.gpsimd, older, 10, 6)
                multiply(nc.vector, older, 0, 2)
            maximum_of_bank(unit, 2)
            if slot < 2:
                quantise_support(1, slot + 2)
            if live_older:
                multiply(nc.vector, older, 2, 2)
                add_strips(older, 0, 10)
            maximum_of_bank(unit, 3)
            if slot < 3:
                quantise_keys(1, slot, late_keys[slot])
            maximum_of_four(unit)
            subtract(nc.gpsimd, unit, 0, bank0_copy[unit])
            if live_last and slot < LAST:
                reciprocal(last)
                reciprocal_back(last)
                reciprocal_out(last)
            if pair is not None:
                weights_out(pair)
            for j in (1, 2, 3):
                subtract(nc.vector, unit, j, banks[unit][j])
            if slot == 2:
                quantise_keys(1, 3, late_keys[3])
            if live_older:
                add_strips(older, 10, 6)
            if unit + 1 < UNITS:
                scores(unit + 1, (1, 2, 3))
            if unit + 2 < UNITS:
                scores(unit + 2, (0,))
            for j in EXP_ORDER:
                exponentials(unit, j)
            if unit + 2 < UNITS:
                copy_bank0(unit + 2)
            if live_last and slot < LAST:
                multiply(nc.gpsimd, last, 4, 6)
            if pair_due(slot, 3) is not None and slot < LAST:
                pair_sum_copy(pair_due(slot, 3))
            values(slot // 4, slot % 4)
            if slot == 4:
                weigh_on_scalar(0, range(0, NS // 2))
            if slot == 5:
                weigh_on_scalar(0, range(NS // 2, NS))
            if slot == 6:
                weigh_on_scalar(1, range(0, LATE_PRODUCTS))
        fold_products(nc.gpsimd, 0, 0, 8)
        keep_warm(2)
        sum_over_images(LAST, EXP_ORDER[:3])
        reciprocal(LAST - 1)
        reciprocal_back(LAST - 1)
        sum_over_images(LAST, EXP_ORDER[3:])
        reciprocal_out(LAST - 1)
        pair_sum_copy(2)
        multiply(nc.gpsimd, LAST - 1, 8, 4)
        multiply(nc.gpsimd, LAST - 1, 12, 4)
        weigh_on_vector(1, range(LATE_PRODUCTS, NS))
        keep_warm(2)
        pair_sum_turn(2)
        weights_out(2)
        add_products(0, range(8), 8)
        reciprocal(LAST)
        reciprocal_back(LAST)
        add_products(1, range(0, 10))
        reciprocal_out(LAST)
        store(0)
        multiply(nc.gpsimd, LAST, 12, 4)
        multiply(nc.vector, LAST - 1, 0, 4)
        multiply(nc.vector, LAST - 1, 4, 4)
        for first in range(0, 12, 4):
            multiply(nc.vector, LAST, first, 4)
        weigh_on_scalar(2, (0, 8, 1, 9, 2, 10, 3, 11, 4, 12, 5, 13, 6, 14, 7, 15))
        fold_products(nc.vector, 2, 0, 4)
        fold_products(nc.vector, 2, 4, 4)
        keep_warm(2)
        add_strips(LAST - 1, 0, STRIPS)
        keep_warm(2)
        add_strips(LAST, 0, STRIPS)
        add_products(1, range(10, NS))
        pair_sum_copy(3)
        store(1)
        keep_warm(2)
        pair_sum_turn(3)
        weights_out(3)
        add_products(2, range(8), 8)
        weigh_on_vector(3, range(0, 11))
        weigh_on_scalar(3, range(11, NS))
        keep_warm(2)
        add_products(3)
        store(2)
        store(3)
